import numpy as np
import ml_dtypes


def mxq(x, axis, fmt="e4m3"):
    dtype, down = {"e4m3": (ml_dtypes.float8_e4m3fn, 7), "e5m2": (ml_dtypes.float8_e5m2, 14)}[fmt]
    v = np.moveaxis(np.asarray(x, np.float32).astype(ml_dtypes.bfloat16).astype(np.float64), axis, -1)
    blocks = v.reshape(v.shape[:-1] + (-1, 32))
    amax = np.abs(blocks).max(-1, keepdims=True)
    byte = np.maximum(np.where(amax > 0, np.frexp(amax)[1] - 1 + 127, 0) - down, 1)
    scale = np.exp2(byte - 127.0)
    codes = (blocks / scale).astype(np.float32).astype(dtype).astype(np.float64)
    return np.moveaxis((codes * scale).reshape(v.shape), -1, axis)


WIDE = False


def mx_kscale(k):
    if not WIDE:
        return np.ones(k)
    levels = np.array([10, -10, 5, -5, 0])
    a = np.random.permutation(np.resize(levels, k // 512 * 4)).reshape(k // 512, 4)
    idx = np.arange(k)
    return np.exp2(a[idx // 512, idx % 128 // 32])


BF16 = ml_dtypes.bfloat16


def bf(x):
    return np.asarray(x, np.float32).astype(BF16)


def f64(x):
    return np.asarray(x).astype(np.float64)


B, D_IN, HID, LAT, NL = 4096, 512, 512, 512, 2
LN_EPS = 1e-5
SCALE_EPS = 1e-5
LAT2 = LAT + LAT


def silu(v):
    return v / (1.0 + np.exp(-v))


def softplus(v):
    return np.maximum(v, 0.0) + np.log(1.0 + np.exp(-np.abs(v)))


def layer_norm(v, g, b):
    m = v.mean(-1, keepdims=True)
    var = np.square(v - m).mean(-1, keepdims=True)
    return (v - m) / np.sqrt(var + LN_EPS) * g + b


def setup_inputs():
    s = mx_kscale(HID)
    return {"h_enc": bf(silu(np.random.standard_normal((B, HID))) * s),
            "noise": bf(np.random.standard_normal((B, LAT))),
            "enc_w_out": bf(np.random.standard_normal((HID, LAT2)) / np.sqrt(HID) / s[:, None]),
            "enc_b_out": bf(0.1 * np.random.standard_normal(LAT2)),
            "dec_w_in": bf(np.random.standard_normal((LAT, HID)) / np.sqrt(LAT)),
            "dec_b_in": bf(0.1 * np.random.standard_normal(HID)),
            "dec_ln_g": bf(1.0 + 0.1 * np.random.standard_normal(HID)),
            "dec_ln_b": bf(0.1 * np.random.standard_normal(HID))}


def reference(h_enc, noise, enc_w_out, enc_b_out, dec_w_in, dec_b_in, dec_ln_g, dec_ln_b):
    enc_out = (mxq(f64(h_enc), 1, "e4m3") @ mxq(f64(enc_w_out), 0, "e4m3")) + f64(enc_b_out)
    mu, log_var = enc_out[:, :LAT], enc_out[:, LAT:]
    scale = softplus(log_var) + SCALE_EPS
    z = mu + scale * f64(noise)
    pre = (mxq(z, 1, "e4m3") @ mxq(f64(dec_w_in), 0, "e4m3")) + f64(dec_b_in)
    h_dec = silu(layer_norm(pre, f64(dec_ln_g), f64(dec_ln_b)))
    kl_row = 0.5 * np.sum(np.square(scale) + np.square(mu) - 1.0, axis=-1) - np.sum(np.log(scale), axis=-1)
    return z, h_dec, kl_row

@@ -1,0 +1,355 @@
+from contextlib import ExitStack
+
+import concourse.mybir as mybir
+from concourse.masks import make_identity
+
+F32 = mybir.dt.float32
+BF16 = mybir.dt.bfloat16
+U32 = mybir.dt.uint32
+U8 = mybir.dt.uint8
+FP8X4 = mybir.dt.float8_e4m3fn_x4
+ALU = mybir.AluOpType
+ACT = mybir.ActivationFunctionType
+
+P = 128
+ROWS = 4096
+D = 512
+NT = ROWS // P
+CH = 4
+NCH = NT // CH
+LN_EPS = 1e-5
+SCALE_EPS = 1e-5
+LN_TOP = 44.0
+
+FLOPS = 2 * ROWS * D * (2 * D) + 2 * ROWS * D * D
+
+
+def tile_latentvaeblock_pa_t_kernel(
+    tc, h_enc, noise, enc_w_out, enc_b_out, dec_w_in, dec_b_in, dec_ln_g, dec_ln_b, out_0, out_1, out_2
+):
+    nc = tc.nc
+    h_v = h_enc.rearrange("(p t) k -> p t k", t=NT)
+    n_v = noise.rearrange("(p t) k -> p t k", t=NT)
+    z_v = out_0.rearrange("(p t) k -> p t k", t=NT)
+    d_v = out_1.rearrange("(p t) k -> p t k", t=NT)
+    kl_v = out_2.rearrange("(p t) -> p t", t=NT)
+
+    with ExitStack() as ctx:
+        ctx.enter_context(tc.manual_schedule())
+        const = ctx.enter_context(tc.tile_pool(name="const", bufs=1))
+        big = ctx.enter_context(tc.tile_pool(name="big", bufs=1))
+        wst = ctx.enter_context(tc.tile_pool(name="wst", bufs=4))
+        hst = ctx.enter_context(tc.tile_pool(name="hst", bufs=4))
+        nst = ctx.enter_context(tc.tile_pool(name="nst", bufs=3))
+        grp = ctx.enter_context(tc.tile_pool(name="grp", bufs=3))
+        mup = ctx.enter_context(tc.tile_pool(name="mup", bufs=3))
+        ps_t = ctx.enter_context(tc.psum_pool(name="ps_t", bufs=3))
+        ps_m = ctx.enter_context(tc.psum_pool(name="ps_m", bufs=5))
+
+        ident = const.tile([P, P], F32, name="ident")
+        make_identity(nc, ident[:])
+        one_t = const.tile([P, 1], F32, name="one_t")
+        eps_t = const.tile([P, 1], F32, name="eps_t")
+        warm = const.tile([P, 1], F32, name="warm")
+        mhalf = const.tile([P, CH], F32, name="mhalf")
+        nc.vector.memset(one_t[:], 1.0)
+        nc.vector.memset(eps_t[:], SCALE_EPS)
+        nc.vector.memset(mhalf[:], -0.5)
+        b_enc = const.tile([P, 2 * D], BF16, name="b_enc")
+        nc.scalar.dma_start(out=b_enc[:], in_=enc_b_out.partition_broadcast(P))
+        nc.scalar.activation(out=warm[:], in_=one_t[:], func=ACT.Exp)
+
+        b_dec = const.tile([P, D], BF16, name="b_dec")
+        g_t = const.tile([P, D], BF16, name="g_t")
+        bln_t = const.tile([P, D], BF16, name="bln_t")
+        w1c = const.tile([P, 2 * D], U32, name="w1c", align_bytes=64)
+        w1s = const.tile([P, 2 * D], U8, name="w1s", align_bytes=64)
+        w2c = const.tile([P, D], U32, name="w2c", align_bytes=64)
+        w2s = const.tile([P, D], U8, name="w2s", align_bytes=64)
+        hc = const.tile([P, NT * P], U32, name="hc", align_bytes=64)
+        hs = const.tile([P, NT * P], U8, name="hs", align_bytes=64)
+        junk = const.tile([P, D], BF16, name="junk")
+        sumln = const.tile([P, NT], F32, name="sumln")
+        sums2 = const.tile([P, NT], F32, name="sums2")
+        summu = const.tile([P, NT], F32, name="summu")
+        sumdev = const.tile([P, NT], F32, name="sumdev")
+        sumpre = const.tile([P, NT], F32, name="sumpre")
+        negmean = const.tile([P, NT], F32, name="negmean")
+        varep = const.tile([P, NT], F32, name="varep")
+        rstd = const.tile([P, NT], F32, name="rstd")
+        kl_a = const.tile([P, NT], F32, name="kl_a")
+        kl_b = const.tile([P, NT], F32, name="kl_b")
+        kl_c = const.tile([P, NT], F32, name="kl_c")
+
+        ta = [big.tile([P, D], F32, name="ta%d" % i) for i in range(NT)]
+        tb = [big.tile([P, D], F32, name="tb%d" % i) for i in range(NT)]
+
+        hch = {}
+        nch = {}
+
+        def load_h(c, parts=1):
+            hch[c] = hst.tile([P, CH, D], BF16, name="hch")
+            step = CH // parts
+            for q in range(parts):
+                nc.sync.dma_start(
+                    out=hch[c][:, q * step : (q + 1) * step, :], in_=h_v[:, c * CH + q * step : c * CH + (q + 1) * step, :]
+                )
+
+        def load_n(c):
+            nch[c] = nst.tile([P, CH, D], BF16, name="nch")
+            nc.sync.dma_start(out=nch[c][:], in_=n_v[:, c * CH : (c + 1) * CH, :])
+
+        wraw = {}
+
+        def load_w1(half):
+            wraw[half] = wst.tile([P, 4, D], BF16, name="wraw", tag="w", align_bytes=64)
+            src = enc_w_out[:, half * D : (half + 1) * D].rearrange("(u p e) c -> u p e c", u=2, e=2)
+            for u in range(2):
+                nc.sync.dma_start(out=wraw[half][:, 2 * u : 2 * u + 2, :], in_=src[u])
+
+        def load_w2():
+            wraw[2] = wst.tile([P, 4, D], BF16, name="wraw", tag="w", align_bytes=64)
+            nc.sync.dma_start(out=wraw[2][:], in_=dec_w_in.rearrange("(t p) n -> p t n", p=P))
+
+        hps = {}
+        hg = {}
+        lvp = {}
+
+        def tr_h(j):
+            hps[j] = ps_t.tile([P, 4, P], F32, name="hps", tag="tr")
+            for jj in range(2):
+                i = 2 * j + jj
+                words = hch[i // CH][:, i % CH, :].bitcast(F32)
+                for u in range(2):
+                    nc.tensor.transpose(hps[j][:, 2 * jj + u, :], words[:, u * P : (u + 1) * P], ident[:])
+
+        def ev_h(j, eng):
+            hg[j] = grp.tile([P, 2, P, 2], F32, name="hg", align_bytes=64)
+            dst = hg[j][:]
+            src = hps[j][:].rearrange("p (j u) r -> p j r u", u=2)
+            if eng == 0:
+                nc.scalar.copy(out=dst, in_=src)
+            else:
+                nc.vector.tensor_copy(out=dst, in_=src)
+
+        def q_h(j):
+            cols = slice(2 * j * P, (2 * j + 2) * P)
+            nc.vector.quantize_mx(
+                out=hc[:, cols].bitcast(FP8X4), scales=hs[:, cols], in_=hg[j][:].rearrange("p j r u -> p (j r u)").bitcast(BF16)
+            )
+
+        def mm1(i, half):
+            acc = ps_m.tile([P, D], F32, name="acc", tag="mm")
+            cols = slice(i * P, (i + 1) * P)
+            wcols = slice(half * D, (half + 1) * D)
+            nc.tensor.matmul_mx(
+                out=acc[:],
+                lhsT=hc[:, cols].bitcast(FP8X4),
+                lhsT_scale=hs[:, cols],
+                rhs=w1c[:, wcols].bitcast(FP8X4),
+                rhs_scale=w1s[:, wcols],
+                start=True,
+                stop=True,
+            )
+            return acc
+
+        def lv_add(i):
+            nc.vector.tensor_tensor(out=ta[i][:], in0=lvp[i][:], in1=b_enc[:, D : 2 * D], op=ALU.add)
+
+        def exp_lv(i):
+            nc.scalar.activation(out=tb[i][:], in_=ta[i][:], func=ACT.Exp)
+
+        def regroup_w(which, eng):
+            wg = wst.tile([P, D, 4], BF16, name="wg", tag="w", align_bytes=64)
+            dst = wg[:].rearrange("p (c i) t -> p c t i", i=4)
+            src = wraw[which][:].rearrange("p t (c i) -> p c t i", i=4)
+            if eng == 0:
+                nc.vector.tensor_copy(out=dst, in_=src)
+            else:
+                nc.gpsimd.tensor_scalar(out=dst, in0=src, scalar1=1.0, scalar2=0.0, op0=ALU.mult, op1=ALU.add)
+            return wg
+
+        def quant_w(wg, codes, scales):
+            nc.vector.quantize_mx(out=codes.bitcast(FP8X4), scales=scales, in_=wg[:].rearrange("p c t -> p (c t)"))
+
+        NP = NT // 2
+        load_w1(1)
+        load_h(0, parts=2)
+        load_h(1)
+        load_h(2)
+        load_h(3)
+        load_w1(0)
+        load_w2()
+        nc.sync.dma_start(out=b_dec[:], in_=dec_b_in.partition_broadcast(P))
+        nc.sync.dma_start(out=g_t[:], in_=dec_ln_g.partition_broadcast(P))
+        nc.sync.dma_start(out=bln_t[:], in_=dec_ln_b.partition_broadcast(P))
+        wg_lv = regroup_w(1, 0)
+        wg_mu = regroup_w(0, 1)
+        for j in range(3):
+            tr_h(j)
+        ev_h(0, 0)
+        quant_w(wg_lv, w1c[:, D : 2 * D], w1s[:, D : 2 * D])
+        ev_h(1, 0)
+        q_h(0)
+        lvp[0] = mm1(0, 1)
+        lvp[1] = mm1(1, 1)
+        load_h(4)
+        wg_w2 = regroup_w(2, 1)
+        for j in range(NP + 1):
+            if j + 3 < NP:
+                tr_h(j + 3)
+                if j % 2 == 0 and (j + 3) // 2 + 4 < NCH:
+                    load_h((j + 3) // 2 + 4)
+            if j + 2 < NP:
+                ev_h(j + 2, 1 if j % 4 == 3 else 0)
+            if j + 1 < NP:
+                q_h(j + 1)
+                lvp[2 * j + 2] = mm1(2 * j + 2, 1)
+                lvp[2 * j + 3] = mm1(2 * j + 3, 1)
+            if j < NP:
+                lv_add(2 * j)
+                lv_add(2 * j + 1)
+            if j >= 1:
+                exp_lv(2 * j - 2)
+                exp_lv(2 * j - 1)
+            if j == 10:
+                load_n(0)
+            if j == 12:
+                load_n(1)
+        quant_w(wg_mu, w1c[:, 0:D], w1s[:, 0:D])
+        quant_w(wg_w2, w2c[:], w2s[:])
+
+        mps = {}
+        mu = {}
+        zps = {}
+        zg = {}
+        zc = {}
+        zs = {}
+        pps = {}
+
+        def mu_add(i):
+            mu[i] = mup.tile([P, D], F32, name="mu")
+            nc.vector.tensor_tensor(out=mu[i][:], in0=mps[i][:], in1=b_enc[:, 0:D], op=ALU.add)
+
+        def ln1(i):
+            nc.scalar.activation(out=tb[i][:], in_=tb[i][:], func=ACT.Ln, bias=one_t[:])
+
+        def softplus_guard(i):
+            nc.vector.scalar_tensor_tensor(out=tb[i][:], in0=tb[i][:], scalar=LN_TOP, in1=ta[i][:], op0=ALU.min, op1=ALU.max)
+
+        def kl_scale_sums(i):
+            nc.scalar.activation(out=junk[:], in_=tb[i][:], func=ACT.Ln, bias=eps_t[:], accum_out=sumln[:, i : i + 1])
+            nc.scalar.activation(out=junk[:], in_=tb[i][:], func=ACT.Square, bias=eps_t[:], accum_out=sums2[:, i : i + 1])
+
+        def kl_mu_sum(i):
+            nc.scalar.activation(out=junk[:], in_=mu[i][:], func=ACT.Square, accum_out=summu[:, i : i + 1])
+
+        def sample(i):
+            nc.vector.scalar_tensor_tensor(
+                out=ta[i][:], in0=tb[i][:], scalar=SCALE_EPS, in1=nch[i // CH][:, i % CH, :], op0=ALU.add, op1=ALU.mult
+            )
+            nc.vector.tensor_tensor(out=ta[i][:], in0=ta[i][:], in1=mu[i][:], op=ALU.add)
+            nc.sync.dma_start(out=z_v[:, i, :], in_=ta[i][:])
+
+        def tr_z(i):
+            zps[i] = ps_t.tile([P, 4, P], F32, name="zps", tag="tr")
+            for t in range(4):
+                nc.tensor.transpose(zps[i][:, t, :], ta[i][:, t * P : (t + 1) * P], ident[:])
+
+        def ev_z(i):
+            zg[i] = grp.tile([P, P, 4], BF16, name="zg", align_bytes=64)
+            nc.scalar.copy(out=zg[i][:], in_=zps[i][:].rearrange("p t r -> p r t"))
+
+        def q_z(i):
+            zc[i] = grp.tile([P, P], U32, name="zc", align_bytes=64)
+            zs[i] = grp.tile([P, P], U8, name="zs", align_bytes=64)
+            nc.vector.quantize_mx(out=zc[i][:].bitcast(FP8X4), scales=zs[i][:], in_=zg[i][:].rearrange("p r t -> p (r t)"))
+
+        def mm2(i):
+            pps[i] = ps_m.tile([P, D], F32, name="acc", tag="mm")
+            nc.tensor.matmul_mx(
+                out=pps[i][:],
+                lhsT=zc[i][:].bitcast(FP8X4),
+                lhsT_scale=zs[i][:],
+                rhs=w2c[:].bitcast(FP8X4),
+                rhs_scale=w2s[:],
+                start=True,
+                stop=True,
+            )
+
+        def pre_add(i):
+            nc.vector.scalar_tensor_tensor(
+                out=tb[i][:], in0=pps[i][:], scalar=0.0, in1=b_dec[:], op0=ALU.add, op1=ALU.add, accum_out=sumpre[:, i : i + 1]
+            )
+            nc.gpsimd.tensor_scalar(
+                out=negmean[:, i : i + 1], in0=sumpre[:, i : i + 1], scalar1=-1.0 / D, scalar2=0.0, op0=ALU.mult, op1=ALU.add
+            )
+
+        mps[0] = mm1(0, 0)
+        ln1(0)
+        mu_add(0)
+        for k in range(NT + 2):
+            if k + 1 < NT:
+                mps[k + 1] = mm1(k + 1, 0)
+                ln1(k + 1)
+            if 0 <= k - 1 < NT:
+                ev_z(k - 1)
+            if k < NT:
+                if k % CH == 0 and k // CH + 2 < NCH:
+                    load_n(k // CH + 2)
+                kl_mu_sum(k)
+                softplus_guard(k)
+                kl_scale_sums(k)
+                sample(k)
+                tr_z(k)
+            if 0 <= k - 1 < NT:
+                q_z(k - 1)
+                mm2(k - 1)
+            if k + 1 < NT:
+                mu_add(k + 1)
+            if 0 <= k - 2 < NT:
+                pre_add(k - 2)
+
+        nc.gpsimd.tensor_tensor(out=kl_a[:], in0=sums2[:], in1=summu[:], op=ALU.add)
+        nc.gpsimd.tensor_scalar(out=kl_b[:], in0=kl_a[:], scalar1=0.5, scalar2=-0.5 * D, op0=ALU.mult, op1=ALU.add)
+        nc.gpsimd.tensor_tensor(out=kl_c[:], in0=kl_b[:], in1=sumln[:], op=ALU.subtract)
+        nc.sync.dma_start(out=kl_v, in_=kl_c[:])
+
+        def sq_dev(i):
+            nc.scalar.activation(
+                out=junk[:], in_=tb[i][:], func=ACT.Square, bias=negmean[:, i : i + 1], accum_out=sumdev[:, i : i + 1]
+            )
+            if i % CH == CH - 1:
+                cols = slice(i + 1 - CH, i + 1)
+                nc.gpsimd.tensor_scalar(
+                    out=varep[:, cols], in0=sumdev[:, cols], scalar1=1.0 / D, scalar2=LN_EPS, op0=ALU.mult, op1=ALU.add
+                )
+                nc.gpsimd.tensor_tensor(out=rstd[:, cols], in0=varep[:, cols], in1=mhalf[:], op=ALU.pow)
+
+        def centre(i):
+            nc.vector.scalar_tensor_tensor(
+                out=tb[i][:], in0=tb[i][:], scalar=negmean[:, i : i + 1], in1=g_t[:], op0=ALU.add, op1=ALU.mult
+            )
+
+        def affine(i):
+            nc.vector.scalar_tensor_tensor(
+                out=tb[i][:], in0=tb[i][:], scalar=rstd[:, i : i + 1], in1=bln_t[:], op0=ALU.mult, op1=ALU.add
+            )
+
+        def silu_store(i):
+            nc.scalar.activation(out=tb[i][:], in_=tb[i][:], func=ACT.Silu)
+            nc.sync.dma_start(out=d_v[:, i, :], in_=tb[i][:])
+
+        LEAD_SQ = 8
+        LEAD_C = 6
+        for i in range(LEAD_SQ):
+            sq_dev(i)
+            if i >= LEAD_SQ - LEAD_C:
+                centre(i - (LEAD_SQ - LEAD_C))
+        for i in range(NT):
+            if i + LEAD_SQ < NT:
+                sq_dev(i + LEAD_SQ)
+            if i + LEAD_C < NT:
+                centre(i + LEAD_C)
+            affine(i)
+            silu_store(i)

@@ -244,10 +244,12 @@ def tile_latentvaeblock_pa_t_kernel(
         def kl_mu_sum(i):
             nc.scalar.activation(out=junk[:], in_=mu[i][:], func=ACT.Square, accum_out=summu[:, i : i + 1])
 
-        def sample(i):
+        def scale_noise(i):
             nc.vector.scalar_tensor_tensor(
                 out=ta[i][:], in0=tb[i][:], scalar=SCALE_EPS, in1=nch[i // CH][:, i % CH, :], op0=ALU.add, op1=ALU.mult
             )
+
+        def sample(i):
             nc.vector.tensor_tensor(out=ta[i][:], in0=ta[i][:], in1=mu[i][:], op=ALU.add)
             nc.sync.dma_start(out=z_v[:, i, :], in_=ta[i][:])
 
@@ -285,30 +287,39 @@ def tile_latentvaeblock_pa_t_kernel(
                 out=negmean[:, i : i + 1], in0=sumpre[:, i : i + 1], scalar1=-1.0 / D, scalar2=0.0, op0=ALU.mult, op1=ALU.add
             )
 
+        def on(i):
+            return 0 <= i < NT
+
         mps[0] = mm1(0, 0)
+        mps[1] = mm1(1, 0)
         ln1(0)
         mu_add(0)
-        for k in range(NT + 2):
-            if k + 1 < NT:
-                mps[k + 1] = mm1(k + 1, 0)
+        for k in range(NT + 3):
+            if on(k - 1):
+                tr_z(k - 1)
+            if on(k + 2):
+                mps[k + 2] = mm1(k + 2, 0)
+            if on(k + 1):
                 ln1(k + 1)
-            if 0 <= k - 1 < NT:
-                ev_z(k - 1)
-            if k < NT:
+            if on(k):
                 if k % CH == 0 and k // CH + 2 < NCH:
                     load_n(k // CH + 2)
                 kl_mu_sum(k)
                 softplus_guard(k)
-                kl_scale_sums(k)
-                sample(k)
-                tr_z(k)
-            if 0 <= k - 1 < NT:
-                q_z(k - 1)
-                mm2(k - 1)
-            if k + 1 < NT:
+            if on(k + 1):
                 mu_add(k + 1)
-            if 0 <= k - 2 < NT:
-                pre_add(k - 2)
+            if on(k):
+                kl_scale_sums(k)
+                scale_noise(k)
+            if on(k - 3):
+                pre_add(k - 3)
+            if on(k):
+                sample(k)
+            if on(k - 1):
+                ev_z(k - 1)
+            if on(k - 2):
+                q_z(k - 2)
+                mm2(k - 2)
 
         nc.gpsimd.tensor_tensor(out=kl_a[:], in0=sums2[:], in1=summu[:], op=ALU.add)
         nc.gpsimd.tensor_scalar(out=kl_b[:], in0=kl_a[:], scalar1=0.5, scalar2=-0.5 * D, op0=ALU.mult, op1=ALU.add)

@@ -43,8 +43,9 @@ def tile_latentvaeblock_pa_t_kernel(
         nst = ctx.enter_context(tc.tile_pool(name="nst", bufs=3))
         grp = ctx.enter_context(tc.tile_pool(name="grp", bufs=3))
         mup = ctx.enter_context(tc.tile_pool(name="mup", bufs=3))
-        ps_t = ctx.enter_context(tc.psum_pool(name="ps_t", bufs=3))
-        ps_m = ctx.enter_context(tc.psum_pool(name="ps_m", bufs=5))
+        ps_t = ctx.enter_context(tc.psum_pool(name="ps_t", bufs=2))
+        ps_m = ctx.enter_context(tc.psum_pool(name="ps_m", bufs=4))
+        ps_c = ctx.enter_context(tc.psum_pool(name="ps_c", bufs=1))
 
         ident = const.tile([P, P], F32, name="ident")
         make_identity(nc, ident[:])
@@ -60,8 +61,12 @@ def tile_latentvaeblock_pa_t_kernel(
         nc.scalar.activation(out=warm[:], in_=one_t[:], func=ACT.Exp)
 
         b_dec = const.tile([P, D], BF16, name="b_dec")
-        g_t = const.tile([P, D], BF16, name="g_t")
-        bln_t = const.tile([P, D], BF16, name="bln_t")
+        g_row = const.tile([P, D], BF16, name="g_row")
+        b_row = const.tile([P, D], BF16, name="b_row")
+        ones = const.tile([P, P], BF16, name="ones")
+        nc.vector.memset(g_row[:], 0.0)
+        nc.vector.memset(b_row[:], 0.0)
+        nc.vector.memset(ones[:], 1.0)
         w1c = const.tile([P, 2 * D], U32, name="w1c", align_bytes=64)
         w1s = const.tile([P, 2 * D], U8, name="w1s", align_bytes=64)
         w2c = const.tile([P, D], U32, name="w2c", align_bytes=64)
@@ -181,27 +186,26 @@ def tile_latentvaeblock_pa_t_kernel(
         load_w1(0)
         load_w2()
         nc.sync.dma_start(out=b_dec[:], in_=dec_b_in.partition_broadcast(P))
-        nc.sync.dma_start(out=g_t[:], in_=dec_ln_g.partition_broadcast(P))
-        nc.sync.dma_start(out=bln_t[:], in_=dec_ln_b.partition_broadcast(P))
+        nc.sync.dma_start(out=g_row[0:1, :], in_=dec_ln_g.rearrange("(o n) -> o n", o=1))
+        nc.sync.dma_start(out=b_row[0:1, :], in_=dec_ln_b.rearrange("(o n) -> o n", o=1))
         wg_lv = regroup_w(1, 0)
-        wg_mu = regroup_w(0, 1)
-        for j in range(3):
-            tr_h(j)
+        tr_h(0)
+        tr_h(1)
         ev_h(0, 0)
+        tr_h(2)
         quant_w(wg_lv, w1c[:, D : 2 * D], w1s[:, D : 2 * D])
         ev_h(1, 0)
         q_h(0)
         lvp[0] = mm1(0, 1)
         lvp[1] = mm1(1, 1)
         load_h(4)
-        wg_w2 = regroup_w(2, 1)
         for j in range(NP + 1):
             if j + 3 < NP:
                 tr_h(j + 3)
                 if j % 2 == 0 and (j + 3) // 2 + 4 < NCH:
                     load_h((j + 3) // 2 + 4)
             if j + 2 < NP:
-                ev_h(j + 2, 1 if j % 4 == 3 else 0)
+                ev_h(j + 2, 0)
             if j + 1 < NP:
                 q_h(j + 1)
                 lvp[2 * j + 2] = mm1(2 * j + 2, 1)
@@ -212,12 +216,20 @@ def tile_latentvaeblock_pa_t_kernel(
             if j >= 1:
                 exp_lv(2 * j - 2)
                 exp_lv(2 * j - 1)
+            if j == 4:
+                wg_mu = regroup_w(0, 0)
+            if j == 8:
+                wg_w2 = regroup_w(2, 0)
             if j == 10:
                 load_n(0)
             if j == 12:
                 load_n(1)
         quant_w(wg_mu, w1c[:, 0:D], w1s[:, 0:D])
         quant_w(wg_w2, w2c[:], w2s[:])
+        g_ps = ps_c.tile([P, D], F32, name="g_ps")
+        b_ps = ps_c.tile([P, D], F32, name="b_ps")
+        nc.tensor.matmul(out=g_ps[:], lhsT=ones[:], rhs=g_row[:], start=True, stop=True)
+        nc.tensor.matmul(out=b_ps[:], lhsT=ones[:], rhs=b_row[:], start=True, stop=True)
 
         mps = {}
         mu = {}
@@ -283,12 +295,52 @@ def tile_latentvaeblock_pa_t_kernel(
             nc.vector.scalar_tensor_tensor(
                 out=tb[i][:], in0=pps[i][:], scalar=0.0, in1=b_dec[:], op0=ALU.add, op1=ALU.add, accum_out=sumpre[:, i : i + 1]
             )
-            nc.gpsimd.tensor_scalar(
-                out=negmean[:, i : i + 1], in0=sumpre[:, i : i + 1], scalar1=-1.0 / D, scalar2=0.0, op0=ALU.mult, op1=ALU.add
+            if i % NEG == NEG - 1:
+                cols = slice(i + 1 - NEG, i + 1)
+                nc.scalar.mul(out=negmean[:, cols], in_=sumpre[:, cols], mul=-1.0 / D)
+
+        NEG = 8
+
+        def sq_dev(i):
+            nc.scalar.activation(
+                out=junk[:], in_=tb[i][:], func=ACT.Square, bias=negmean[:, i : i + 1], accum_out=sumdev[:, i : i + 1]
             )
+            if i % CH == CH - 1:
+                cols = slice(i + 1 - CH, i + 1)
+                nc.gpsimd.tensor_scalar(
+                    out=varep[:, cols], in0=sumdev[:, cols], scalar1=1.0 / D, scalar2=LN_EPS, op0=ALU.mult, op1=ALU.add
+                )
+                nc.gpsimd.tensor_tensor(out=rstd[:, cols], in0=varep[:, cols], in1=mhalf[:], op=ALU.pow)
+
+        def centre(i):
+            nc.vector.scalar_tensor_tensor(
+                out=tb[i][:], in0=tb[i][:], scalar=negmean[:, i : i + 1], in1=g_ps[:], op0=ALU.add, op1=ALU.mult
+            )
+
+        def affine(i):
+            nc.vector.scalar_tensor_tensor(
+                out=tb[i][:], in0=tb[i][:], scalar=rstd[:, i : i + 1], in1=b_ps[:], op0=ALU.mult, op1=ALU.add
+            )
+
+        def silu_store(i):
+            nc.scalar.activation(out=tb[i][:], in_=tb[i][:], func=ACT.Silu)
+            nc.sync.dma_start(out=d_v[:, i, :], in_=tb[i][:])
+
+        LEAD_SQ = 8
+        LEAD_C = 6
+        EARLY = 3
 
         def on(i):
             return 0 <= i < NT
+
+        def step3(n):
+            if on(n):
+                sq_dev(n)
+            if on(n - (LEAD_SQ - LEAD_C)):
+                centre(n - (LEAD_SQ - LEAD_C))
+            if on(n - LEAD_SQ):
+                affine(n - LEAD_SQ)
+                silu_store(n - LEAD_SQ)
 
         mps[0] = mm1(0, 0)
         mps[1] = mm1(1, 0)
@@ -320,47 +372,14 @@ def tile_latentvaeblock_pa_t_kernel(
             if on(k - 2):
                 q_z(k - 2)
                 mm2(k - 2)
+            if k >= NT:
+                for n in range(EARLY * (k - NT), EARLY * (k - NT + 1)):
+                    step3(n)
 
         nc.gpsimd.tensor_tensor(out=kl_a[:], in0=sums2[:], in1=summu[:], op=ALU.add)
         nc.gpsimd.tensor_scalar(out=kl_b[:], in0=kl_a[:], scalar1=0.5, scalar2=-0.5 * D, op0=ALU.mult, op1=ALU.add)
         nc.gpsimd.tensor_tensor(out=kl_c[:], in0=kl_b[:], in1=sumln[:], op=ALU.subtract)
         nc.sync.dma_start(out=kl_v, in_=kl_c[:])
 
-        def sq_dev(i):
-            nc.scalar.activation(
-                out=junk[:], in_=tb[i][:], func=ACT.Square, bias=negmean[:, i : i + 1], accum_out=sumdev[:, i : i + 1]
-            )
-            if i % CH == CH - 1:
-                cols = slice(i + 1 - CH, i + 1)
-                nc.gpsimd.tensor_scalar(
-                    out=varep[:, cols], in0=sumdev[:, cols], scalar1=1.0 / D, scalar2=LN_EPS, op0=ALU.mult, op1=ALU.add
-                )
-                nc.gpsimd.tensor_tensor(out=rstd[:, cols], in0=varep[:, cols], in1=mhalf[:], op=ALU.pow)
-
-        def centre(i):
-            nc.vector.scalar_tensor_tensor(
-                out=tb[i][:], in0=tb[i][:], scalar=negmean[:, i : i + 1], in1=g_t[:], op0=ALU.add, op1=ALU.mult
-            )
-
-        def affine(i):
-            nc.vector.scalar_tensor_tensor(
-                out=tb[i][:], in0=tb[i][:], scalar=rstd[:, i : i + 1], in1=bln_t[:], op0=ALU.mult, op1=ALU.add
-            )
-
-        def silu_store(i):
-            nc.scalar.activation(out=tb[i][:], in_=tb[i][:], func=ACT.Silu)
-            nc.sync.dma_start(out=d_v[:, i, :], in_=tb[i][:])
-
-        LEAD_SQ = 8
-        LEAD_C = 6
-        for i in range(LEAD_SQ):
-            sq_dev(i)
-            if i >= LEAD_SQ - LEAD_C:
-                centre(i - (LEAD_SQ - LEAD_C))
-        for i in range(NT):
-            if i + LEAD_SQ < NT:
-                sq_dev(i + LEAD_SQ)
-            if i + LEAD_C < NT:
-                centre(i + LEAD_C)
-            affine(i)
-            silu_store(i)
+        for n in range(3 * EARLY, NT + LEAD_SQ):
+            step3(n)

@@ -44,7 +44,7 @@ def tile_latentvaeblock_pa_t_kernel(
         grp = ctx.enter_context(tc.tile_pool(name="grp", bufs=3))
         mup = ctx.enter_context(tc.tile_pool(name="mup", bufs=3))
         ps_t = ctx.enter_context(tc.psum_pool(name="ps_t", bufs=2))
-        ps_m = ctx.enter_context(tc.psum_pool(name="ps_m", bufs=4))
+        ps_m = ctx.enter_context(tc.psum_pool(name="ps_m", bufs=2))
         ps_c = ctx.enter_context(tc.psum_pool(name="ps_c", bufs=1))
 
         ident = const.tile([P, P], F32, name="ident")
@@ -143,8 +143,8 @@ def tile_latentvaeblock_pa_t_kernel(
                 out=hc[:, cols].bitcast(FP8X4), scales=hs[:, cols], in_=hg[j][:].rearrange("p j r u -> p (j r u)").bitcast(BF16)
             )
 
-        def mm1(i, half):
-            acc = ps_m.tile([P, D], F32, name="acc", tag="mm")
+        def mm1(i, half, tag):
+            acc = ps_m.tile([P, D], F32, name="acc", tag=tag)
             cols = slice(i * P, (i + 1) * P)
             wcols = slice(half * D, (half + 1) * D)
             nc.tensor.matmul_mx(
@@ -196,8 +196,8 @@ def tile_latentvaeblock_pa_t_kernel(
         quant_w(wg_lv, w1c[:, D : 2 * D], w1s[:, D : 2 * D])
         ev_h(1, 0)
         q_h(0)
-        lvp[0] = mm1(0, 1)
-        lvp[1] = mm1(1, 1)
+        lvp[0] = mm1(0, 1, "m1")
+        lvp[1] = mm1(1, 1, "m1")
         load_h(4)
         for j in range(NP + 1):
             if j + 3 < NP:
@@ -208,8 +208,8 @@ def tile_latentvaeblock_pa_t_kernel(
                 ev_h(j + 2, 0)
             if j + 1 < NP:
                 q_h(j + 1)
-                lvp[2 * j + 2] = mm1(2 * j + 2, 1)
-                lvp[2 * j + 3] = mm1(2 * j + 3, 1)
+                lvp[2 * j + 2] = mm1(2 * j + 2, 1, "m2" if j % 2 == 0 else "m1")
+                lvp[2 * j + 3] = mm1(2 * j + 3, 1, "m2" if j % 2 == 0 else "m1")
             if j < NP:
                 lv_add(2 * j)
                 lv_add(2 * j + 1)
@@ -280,7 +280,7 @@ def tile_latentvaeblock_pa_t_kernel(
             nc.vector.quantize_mx(out=zc[i][:].bitcast(FP8X4), scales=zs[i][:], in_=zg[i][:].rearrange("p r t -> p (r t)"))
 
         def mm2(i):
-            pps[i] = ps_m.tile([P, D], F32, name="acc", tag="mm")
+            pps[i] = ps_m.tile([P, D], F32, name="acc", tag="m2")
             nc.tensor.matmul_mx(
                 out=pps[i][:],
                 lhsT=zc[i][:].bitcast(FP8X4),
@@ -340,19 +340,24 @@ def tile_latentvaeblock_pa_t_kernel(
                 centre(n - (LEAD_SQ - LEAD_C))
             if on(n - LEAD_SQ):
                 affine(n - LEAD_SQ)
-                silu_store(n - LEAD_SQ)
+            if on(n - LEAD_SQ - 1):
+                silu_store(n - LEAD_SQ - 1)
 
-        mps[0] = mm1(0, 0)
-        mps[1] = mm1(1, 0)
+        mps[0] = mm1(0, 0, "m1")
+        mps[1] = mm1(1, 0, "m1")
         ln1(0)
         mu_add(0)
-        for k in range(NT + 3):
+        mps[2] = mm1(2, 0, "m1")
+        DRAIN = 4
+        for k in range(NT + DRAIN):
             if on(k - 1):
                 tr_z(k - 1)
-            if on(k + 2):
-                mps[k + 2] = mm1(k + 2, 0)
+            if on(k - 3):
+                mm2(k - 3)
             if on(k + 1):
                 ln1(k + 1)
+            if on(k - 1):
+                kl_scale_sums(k - 1)
             if on(k):
                 if k % CH == 0 and k // CH + 2 < NCH:
                     load_n(k // CH + 2)
@@ -360,18 +365,18 @@ def tile_latentvaeblock_pa_t_kernel(
                 softplus_guard(k)
             if on(k + 1):
                 mu_add(k + 1)
+            if on(k + 3):
+                mps[k + 3] = mm1(k + 3, 0, "m1")
             if on(k):
-                kl_scale_sums(k)
                 scale_noise(k)
-            if on(k - 3):
-                pre_add(k - 3)
+            if on(k - 4):
+                pre_add(k - 4)
             if on(k):
                 sample(k)
             if on(k - 1):
                 ev_z(k - 1)
             if on(k - 2):
                 q_z(k - 2)
-                mm2(k - 2)
             if k >= NT:
                 for n in range(EARLY * (k - NT), EARLY * (k - NT + 1)):
                     step3(n)
@@ -381,5 +386,5 @@ def tile_latentvaeblock_pa_t_kernel(
         nc.gpsimd.tensor_tensor(out=kl_c[:], in0=kl_b[:], in1=sumln[:], op=ALU.subtract)
         nc.sync.dma_start(out=kl_v, in_=kl_c[:])
 
-        for n in range(3 * EARLY, NT + LEAD_SQ):
+        for n in range(DRAIN * EARLY, NT + LEAD_SQ + 1):
             step3(n)

@@ -73,7 +73,7 @@ def tile_latentvaeblock_pa_t_kernel(
         w2s = const.tile([P, D], U8, name="w2s", align_bytes=64)
         hc = const.tile([P, NT * P], U32, name="hc", align_bytes=64)
         hs = const.tile([P, NT * P], U8, name="hs", align_bytes=64)
-        junk = const.tile([P, D], BF16, name="junk")
+        junk = [const.tile([P, D], BF16, name="junk%d" % q) for q in range(4)]
         sumln = const.tile([P, NT], F32, name="sumln")
         sums2 = const.tile([P, NT], F32, name="sums2")
         summu = const.tile([P, NT], F32, name="summu")
@@ -250,11 +250,11 @@ def tile_latentvaeblock_pa_t_kernel(
             nc.vector.scalar_tensor_tensor(out=tb[i][:], in0=tb[i][:], scalar=LN_TOP, in1=ta[i][:], op0=ALU.min, op1=ALU.max)
 
         def kl_scale_sums(i):
-            nc.scalar.activation(out=junk[:], in_=tb[i][:], func=ACT.Ln, bias=eps_t[:], accum_out=sumln[:, i : i + 1])
-            nc.scalar.activation(out=junk[:], in_=tb[i][:], func=ACT.Square, bias=eps_t[:], accum_out=sums2[:, i : i + 1])
+            nc.scalar.activation(out=junk[0][:], in_=tb[i][:], func=ACT.Ln, bias=eps_t[:], accum_out=sumln[:, i : i + 1])
+            nc.scalar.activation(out=junk[1][:], in_=tb[i][:], func=ACT.Square, bias=eps_t[:], accum_out=sums2[:, i : i + 1])
 
         def kl_mu_sum(i):
-            nc.scalar.activation(out=junk[:], in_=mu[i][:], func=ACT.Square, accum_out=summu[:, i : i + 1])
+            nc.scalar.activation(out=junk[2][:], in_=mu[i][:], func=ACT.Square, accum_out=summu[:, i : i + 1])
 
         def scale_noise(i):
             nc.vector.scalar_tensor_tensor(
@@ -303,7 +303,7 @@ def tile_latentvaeblock_pa_t_kernel(
 
         def sq_dev(i):
             nc.scalar.activation(
-                out=junk[:], in_=tb[i][:], func=ACT.Square, bias=negmean[:, i : i + 1], accum_out=sumdev[:, i : i + 1]
+                out=junk[i % 4][:], in_=tb[i][:], func=ACT.Square, bias=negmean[:, i : i + 1], accum_out=sumdev[:, i : i + 1]
             )
             if i % CH == CH - 1:
                 cols = slice(i + 1 - CH, i + 1)

@@ -262,7 +262,7 @@ def tile_latentvaeblock_pa_t_kernel(
             )
 
         def sample(i):
-            nc.vector.tensor_tensor(out=ta[i][:], in0=ta[i][:], in1=mu[i][:], op=ALU.add)
+            nc.gpsimd.tensor_tensor(out=ta[i][:], in0=ta[i][:], in1=mu[i][:], op=ALU.add)
             nc.sync.dma_start(out=z_v[:, i, :], in_=ta[i][:])
 
         def tr_z(i):
@@ -272,7 +272,12 @@ def tile_latentvaeblock_pa_t_kernel(
 
         def ev_z(i):
             zg[i] = grp.tile([P, P, 4], BF16, name="zg", align_bytes=64)
-            nc.scalar.copy(out=zg[i][:], in_=zps[i][:].rearrange("p t r -> p r t"))
+            if i % EVZ_MOD == 0:
+                nc.vector.tensor_copy(out=zg[i][:], in_=zps[i][:].rearrange("p t r -> p r t"))
+            else:
+                nc.scalar.copy(out=zg[i][:], in_=zps[i][:].rearrange("p t r -> p r t"))
+
+        EVZ_MOD = 2
 
         def q_z(i):
             zc[i] = grp.tile([P, P], U32, name="zc", align_bytes=64)
@@ -346,37 +351,34 @@ def tile_latentvaeblock_pa_t_kernel(
         mps[0] = mm1(0, 0, "m1")
         mps[1] = mm1(1, 0, "m1")
         ln1(0)
-        mu_add(0)
-        mps[2] = mm1(2, 0, "m1")
-        DRAIN = 4
+        DRAIN = 5
         for k in range(NT + DRAIN):
-            if on(k - 1):
-                tr_z(k - 1)
-            if on(k - 3):
-                mm2(k - 3)
+            if on(k - 2):
+                tr_z(k - 2)
+            if on(k - 4):
+                mm2(k - 4)
             if on(k + 1):
                 ln1(k + 1)
             if on(k - 1):
                 kl_scale_sums(k - 1)
+                kl_mu_sum(k - 1)
             if on(k):
-                if k % CH == 0 and k // CH + 2 < NCH:
-                    load_n(k // CH + 2)
-                kl_mu_sum(k)
                 softplus_guard(k)
-            if on(k + 1):
-                mu_add(k + 1)
-            if on(k + 3):
-                mps[k + 3] = mm1(k + 3, 0, "m1")
-            if on(k):
-                scale_noise(k)
-            if on(k - 4):
-                pre_add(k - 4)
-            if on(k):
-                sample(k)
+            if on(k - 3):
+                q_z(k - 3)
             if on(k - 1):
-                ev_z(k - 1)
+                scale_noise(k - 1)
+                sample(k - 1)
+            if k % CH == 1 and k // CH + 2 < NCH:
+                load_n(k // CH + 2)
+            if on(k):
+                mu_add(k)
+            if on(k + 2):
+                mps[k + 2] = mm1(k + 2, 0, "m1")
+            if on(k - 5):
+                pre_add(k - 5)
             if on(k - 2):
-                q_z(k - 2)
+                ev_z(k - 2)
             if k >= NT:
                 for n in range(EARLY * (k - NT), EARLY * (k - NT + 1)):
                     step3(n)

@@ -15,11 +15,12 @@ P = 128
 ROWS = 4096
 D = 512
 NT = ROWS // P
-CH = 4
-NCH = NT // CH
+G = 4
+NG = NT // G
+NP = NT // 2
 LN_EPS = 1e-5
 SCALE_EPS = 1e-5
-LN_TOP = 44.0
+SIG_FLOOR = 2.0**-62
 
 FLOPS = 2 * ROWS * D * (2 * D) + 2 * ROWS * D * D
 
@@ -42,31 +43,35 @@ def tile_latentvaeblock_pa_t_kernel(
         hst = ctx.enter_context(tc.tile_pool(name="hst", bufs=4))
         nst = ctx.enter_context(tc.tile_pool(name="nst", bufs=3))
         grp = ctx.enter_context(tc.tile_pool(name="grp", bufs=3))
-        mup = ctx.enter_context(tc.tile_pool(name="mup", bufs=3))
-        ps_t = ctx.enter_context(tc.psum_pool(name="ps_t", bufs=2))
-        ps_m = ctx.enter_context(tc.psum_pool(name="ps_m", bufs=2))
-        ps_c = ctx.enter_context(tc.psum_pool(name="ps_c", bufs=1))
+        mup = ctx.enter_context(tc.tile_pool(name="mup", bufs=10))
+        snp = ctx.enter_context(tc.tile_pool(name="snp", bufs=3))
+        ps_lv = ctx.enter_context(tc.psum_pool(name="ps_lv", bufs=2))
+        ps_sr = ctx.enter_context(tc.psum_pool(name="ps_sr", bufs=3))
+        ps_1 = ctx.enter_context(tc.psum_pool(name="ps_1", bufs=1))
 
         ident = const.tile([P, P], F32, name="ident")
         make_identity(nc, ident[:])
+        identb = const.tile([P, P], BF16, name="identb")
+        vecs = const.tile([P, P], BF16, name="vecs")
         one_t = const.tile([P, 1], F32, name="one_t")
         eps_t = const.tile([P, 1], F32, name="eps_t")
         warm = const.tile([P, 1], F32, name="warm")
-        mhalf = const.tile([P, CH], F32, name="mhalf")
+        floor_t = const.tile([P, 1], F32, name="floor_t")
+        mhalf = const.tile([P, G], F32, name="mhalf")
         nc.vector.memset(one_t[:], 1.0)
+        nc.vector.memset(floor_t[:], SIG_FLOOR)
+        nc.vector.memset(vecs[:], 0.0)
         nc.vector.memset(eps_t[:], SCALE_EPS)
         nc.vector.memset(mhalf[:], -0.5)
-        b_enc = const.tile([P, 2 * D], BF16, name="b_enc")
-        nc.scalar.dma_start(out=b_enc[:], in_=enc_b_out.partition_broadcast(P))
-        nc.scalar.activation(out=warm[:], in_=one_t[:], func=ACT.Exp)
+        nc.scalar.dma_start(out=vecs[0:G, :], in_=enc_b_out[D : 2 * D].rearrange("(n p) -> n p", p=P))
+        nc.scalar.activation(out=warm[:], in_=one_t[:], func=ACT.Sigmoid)
+        nc.vector.tensor_copy(out=identb[:], in_=ident[:])
 
+        b_mu = const.tile([P, D], BF16, name="b_mu")
         b_dec = const.tile([P, D], BF16, name="b_dec")
         g_row = const.tile([P, D], BF16, name="g_row")
         b_row = const.tile([P, D], BF16, name="b_row")
-        ones = const.tile([P, P], BF16, name="ones")
-        nc.vector.memset(g_row[:], 0.0)
-        nc.vector.memset(b_row[:], 0.0)
-        nc.vector.memset(ones[:], 1.0)
+        bcol = const.tile([P, G], F32, name="bcol")
         w1c = const.tile([P, 2 * D], U32, name="w1c", align_bytes=64)
         w1s = const.tile([P, 2 * D], U8, name="w1s", align_bytes=64)
         w2c = const.tile([P, D], U32, name="w2c", align_bytes=64)
@@ -86,56 +91,51 @@ def tile_latentvaeblock_pa_t_kernel(
         kl_b = const.tile([P, NT], F32, name="kl_b")
         kl_c = const.tile([P, NT], F32, name="kl_c")
 
-        ta = [big.tile([P, D], F32, name="ta%d" % i) for i in range(NT)]
-        tb = [big.tile([P, D], F32, name="tb%d" % i) for i in range(NT)]
+        et = [big.tile([P, G, D], F32, name="et%d" % g) for g in range(NG)]
+
+        def xrow(i):
+            return et[i // G][:, i % G, :]
 
         hch = {}
         nch = {}
 
         def load_h(c, parts=1):
-            hch[c] = hst.tile([P, CH, D], BF16, name="hch")
-            step = CH // parts
+            hch[c] = hst.tile([P, G, D], BF16, name="hch")
+            step = G // parts
             for q in range(parts):
                 nc.sync.dma_start(
-                    out=hch[c][:, q * step : (q + 1) * step, :], in_=h_v[:, c * CH + q * step : c * CH + (q + 1) * step, :]
+                    out=hch[c][:, q * step : (q + 1) * step, :], in_=h_v[:, c * G + q * step : c * G + (q + 1) * step, :]
                 )
 
         def load_n(c):
-            nch[c] = nst.tile([P, CH, D], BF16, name="nch")
-            nc.sync.dma_start(out=nch[c][:], in_=n_v[:, c * CH : (c + 1) * CH, :])
+            nch[c] = nst.tile([P, G, D], BF16, name="nch")
+            nc.sync.dma_start(out=nch[c][:], in_=n_v[:, c * G : (c + 1) * G, :])
 
         wraw = {}
 
-        def load_w1(half):
-            wraw[half] = wst.tile([P, 4, D], BF16, name="wraw", tag="w", align_bytes=64)
-            src = enc_w_out[:, half * D : (half + 1) * D].rearrange("(u p e) c -> u p e c", u=2, e=2)
+        def load_w(which, w):
+            wraw[which] = wst.tile([P, 4, D], BF16, name="wraw", tag="w", align_bytes=64)
+            src = w.rearrange("(u p e) c -> u p e c", u=2, e=2)
             for u in range(2):
-                nc.sync.dma_start(out=wraw[half][:, 2 * u : 2 * u + 2, :], in_=src[u])
-
-        def load_w2():
-            wraw[2] = wst.tile([P, 4, D], BF16, name="wraw", tag="w", align_bytes=64)
-            nc.sync.dma_start(out=wraw[2][:], in_=dec_w_in.rearrange("(t p) n -> p t n", p=P))
+                nc.sync.dma_start(out=wraw[which][:, 2 * u : 2 * u + 2, :], in_=src[u])
 
         hps = {}
         hg = {}
         lvp = {}
 
+        def tr_words(dst, rows):
+            for u in range(2):
+                nc.tensor.transpose(dst[:, u, :], rows.bitcast(F32)[:, u * P : (u + 1) * P], ident[:])
+
         def tr_h(j):
-            hps[j] = ps_t.tile([P, 4, P], F32, name="hps", tag="tr")
+            hps[j] = ps_1.tile([P, 4, P], F32, name="hps", tag="z" if j % 2 == 0 else "mm2")
             for jj in range(2):
                 i = 2 * j + jj
-                words = hch[i // CH][:, i % CH, :].bitcast(F32)
-                for u in range(2):
-                    nc.tensor.transpose(hps[j][:, 2 * jj + u, :], words[:, u * P : (u + 1) * P], ident[:])
+                tr_words(hps[j][:, 2 * jj : 2 * jj + 2, :], hch[i // G][:, i % G, :])
 
-        def ev_h(j, eng):
+        def ev_h(j):
             hg[j] = grp.tile([P, 2, P, 2], F32, name="hg", align_bytes=64)
-            dst = hg[j][:]
-            src = hps[j][:].rearrange("p (j u) r -> p j r u", u=2)
-            if eng == 0:
-                nc.scalar.copy(out=dst, in_=src)
-            else:
-                nc.vector.tensor_copy(out=dst, in_=src)
+            nc.vector.tensor_copy(out=hg[j][:], in_=hps[j][:].rearrange("p (j u) r -> p j r u", u=2))
 
         def q_h(j):
             cols = slice(2 * j * P, (2 * j + 2) * P)
@@ -143,175 +143,197 @@ def tile_latentvaeblock_pa_t_kernel(
                 out=hc[:, cols].bitcast(FP8X4), scales=hs[:, cols], in_=hg[j][:].rearrange("p j r u -> p (j r u)").bitcast(BF16)
             )
 
-        def mm1(i, half, tag):
-            acc = ps_m.tile([P, D], F32, name="acc", tag=tag)
-            cols = slice(i * P, (i + 1) * P)
-            wcols = slice(half * D, (half + 1) * D)
+        def mx(out, lc, ls, rc, rs):
             nc.tensor.matmul_mx(
-                out=acc[:],
-                lhsT=hc[:, cols].bitcast(FP8X4),
-                lhsT_scale=hs[:, cols],
-                rhs=w1c[:, wcols].bitcast(FP8X4),
-                rhs_scale=w1s[:, wcols],
-                start=True,
-                stop=True,
+                out=out, lhsT=lc.bitcast(FP8X4), lhsT_scale=ls, rhs=rc.bitcast(FP8X4), rhs_scale=rs, start=True, stop=True
             )
-            return acc
 
-        def lv_add(i):
-            nc.vector.tensor_tensor(out=ta[i][:], in0=lvp[i][:], in1=b_enc[:, D : 2 * D], op=ALU.add)
+        def mm_lv(u, pool, tag):
+            lvp[u] = pool.tile([P, D], F32, name="acc", tag=tag)
+            wcols = slice(D + (u % G) * P, D + (u % G + 1) * P)
+            rows = slice((u // G) * G * P, (u // G + 1) * G * P)
+            mx(lvp[u][:], w1c[:, wcols], w1s[:, wcols], hc[:, rows], hs[:, rows])
 
-        def exp_lv(i):
-            nc.scalar.activation(out=tb[i][:], in_=ta[i][:], func=ACT.Exp)
+        def exp_lv(u):
+            n = u % G
+            nc.scalar.activation(out=et[u // G][:, n, :], in_=lvp[u][:], func=ACT.Sigmoid, bias=bcol[:, n : n + 1])
 
-        def regroup_w(which, eng):
+        def pair(u):
+            return et[u // G][:, u % G : u % G + 2, :].rearrange("p a c -> p (a c)")
+
+        def regroup_w(which):
             wg = wst.tile([P, D, 4], BF16, name="wg", tag="w", align_bytes=64)
             dst = wg[:].rearrange("p (c i) t -> p c t i", i=4)
             src = wraw[which][:].rearrange("p t (c i) -> p c t i", i=4)
-            if eng == 0:
-                nc.vector.tensor_copy(out=dst, in_=src)
+            if which == "lv":
+                nc.vector.tensor_scalar(out=dst, in0=src, scalar1=-1.0, scalar2=None, op0=ALU.mult)
             else:
-                nc.gpsimd.tensor_scalar(out=dst, in0=src, scalar1=1.0, scalar2=0.0, op0=ALU.mult, op1=ALU.add)
+                nc.vector.tensor_copy(out=dst, in_=src)
             return wg
 
         def quant_w(wg, codes, scales):
             nc.vector.quantize_mx(out=codes.bitcast(FP8X4), scales=scales, in_=wg[:].rearrange("p c t -> p (c t)"))
 
-        NP = NT // 2
-        load_w1(1)
+        load_w("lv", enc_w_out[:, D : 2 * D])
         load_h(0, parts=2)
         load_h(1)
         load_h(2)
         load_h(3)
-        load_w1(0)
-        load_w2()
+        load_w("mu", enc_w_out[:, 0:D])
+        load_w("dec", dec_w_in)
+        nc.sync.dma_start(out=b_mu[:], in_=enc_b_out[0:D].partition_broadcast(P))
         nc.sync.dma_start(out=b_dec[:], in_=dec_b_in.partition_broadcast(P))
-        nc.sync.dma_start(out=g_row[0:1, :], in_=dec_ln_g.rearrange("(o n) -> o n", o=1))
-        nc.sync.dma_start(out=b_row[0:1, :], in_=dec_ln_b.rearrange("(o n) -> o n", o=1))
-        wg_lv = regroup_w(1, 0)
+        nc.sync.dma_start(out=g_row[:], in_=dec_ln_g.partition_broadcast(P))
+        nc.sync.dma_start(out=b_row[:], in_=dec_ln_b.partition_broadcast(P))
+        wg_lv = regroup_w("lv")
         tr_h(0)
         tr_h(1)
-        ev_h(0, 0)
-        tr_h(2)
         quant_w(wg_lv, w1c[:, D : 2 * D], w1s[:, D : 2 * D])
-        ev_h(1, 0)
+        ev_h(0)
+        tr_h(2)
+        ev_h(1)
         q_h(0)
-        lvp[0] = mm1(0, 1, "m1")
-        lvp[1] = mm1(1, 1, "m1")
+        tr_h(3)
+        bps = ps_1.tile([P, P], BF16, name="bps", tag="mu")
+        nc.tensor.transpose(bps[:], vecs[:], identb[:])
+        nc.vector.tensor_scalar(out=bcol[:], in0=bps[:, 0:G], scalar1=-1.0, scalar2=None, op0=ALU.mult)
+        q_h(1)
+        mm_lv(0, ps_lv, "lv")
+        mm_lv(1, ps_lv, "lv")
+        ev_h(2)
         load_h(4)
-        for j in range(NP + 1):
+        for j in range(NP):
+            if j + 4 < NP:
+                tr_h(j + 4)
+                if j % 2 == 0 and j // 2 + 5 < NG:
+                    load_h(j // 2 + 5)
             if j + 3 < NP:
-                tr_h(j + 3)
-                if j % 2 == 0 and (j + 3) // 2 + 4 < NCH:
-                    load_h((j + 3) // 2 + 4)
+                ev_h(j + 3)
             if j + 2 < NP:
-                ev_h(j + 2, 0)
+                q_h(j + 2)
             if j + 1 < NP:
-                q_h(j + 1)
-                lvp[2 * j + 2] = mm1(2 * j + 2, 1, "m2" if j % 2 == 0 else "m1")
-                lvp[2 * j + 3] = mm1(2 * j + 3, 1, "m2" if j % 2 == 0 else "m1")
-            if j < NP:
-                lv_add(2 * j)
-                lv_add(2 * j + 1)
-            if j >= 1:
-                exp_lv(2 * j - 2)
-                exp_lv(2 * j - 1)
-            if j == 4:
-                wg_mu = regroup_w(0, 0)
-            if j == 8:
-                wg_w2 = regroup_w(2, 0)
+                for u in (2 * j + 2, 2 * j + 3):
+                    if j % 2 == 1:
+                        mm_lv(u, ps_lv, "lv")
+                    else:
+                        mm_lv(u, ps_sr, "sr")
+            exp_lv(2 * j)
+            exp_lv(2 * j + 1)
+            if j == 3:
+                wg_mu = regroup_w("mu")
+            if j == 5:
+                quant_w(wg_mu, w1c[:, 0:D], w1s[:, 0:D])
+            if j == 7:
+                wg_w2 = regroup_w("dec")
+            if j == 9:
+                quant_w(wg_w2, w2c[:], w2s[:])
             if j == 10:
                 load_n(0)
             if j == 12:
                 load_n(1)
-        quant_w(wg_mu, w1c[:, 0:D], w1s[:, 0:D])
-        quant_w(wg_w2, w2c[:], w2s[:])
-        g_ps = ps_c.tile([P, D], F32, name="g_ps")
-        b_ps = ps_c.tile([P, D], F32, name="b_ps")
-        nc.tensor.matmul(out=g_ps[:], lhsT=ones[:], rhs=g_row[:], start=True, stop=True)
-        nc.tensor.matmul(out=b_ps[:], lhsT=ones[:], rhs=b_row[:], start=True, stop=True)
 
-        mps = {}
+        mup_ps = {}
         mu = {}
+        srow = {}
+        sn = {}
+        zt = {}
+        zb = {}
         zps = {}
         zg = {}
         zc = {}
         zs = {}
         pps = {}
 
+        def ln1(u):
+            nc.scalar.activation(out=pair(u), in_=pair(u), func=ACT.Ln, bias=floor_t[:])
+
+        def guard(u):
+            n = u % G
+            dst = et[u // G][:, n, :]
+            nc.vector.scalar_tensor_tensor(
+                out=dst, in0=lvp[u][:], scalar=bcol[:, n : n + 1], in1=dst, op0=ALU.add, op1=ALU.min
+            )
+
+        def tr_s(i):
+            srow[i] = ps_sr.tile([P, D], F32, name="srow", tag="sr")
+            for n in range(G):
+                nc.tensor.transpose(
+                    srow[i][:, n * P : (n + 1) * P], et[i // G][:, n, (i % G) * P : (i % G + 1) * P], ident[:]
+                )
+
+        def mm_mu(i):
+            mup_ps[i] = ps_1.tile([P, D], F32, name="accmu", tag="mu")
+            cols = slice(i * P, (i + 1) * P)
+            mx(mup_ps[i][:], hc[:, cols], hs[:, cols], w1c[:, 0:D], w1s[:, 0:D])
+
         def mu_add(i):
             mu[i] = mup.tile([P, D], F32, name="mu")
-            nc.vector.tensor_tensor(out=mu[i][:], in0=mps[i][:], in1=b_enc[:, 0:D], op=ALU.add)
-
-        def ln1(i):
-            nc.scalar.activation(out=tb[i][:], in_=tb[i][:], func=ACT.Ln, bias=one_t[:])
-
-        def softplus_guard(i):
-            nc.vector.scalar_tensor_tensor(out=tb[i][:], in0=tb[i][:], scalar=LN_TOP, in1=ta[i][:], op0=ALU.min, op1=ALU.max)
+            nc.vector.tensor_tensor(out=mu[i][:], in0=mup_ps[i][:], in1=b_mu[:], op=ALU.add)
 
         def kl_scale_sums(i):
-            nc.scalar.activation(out=junk[0][:], in_=tb[i][:], func=ACT.Ln, bias=eps_t[:], accum_out=sumln[:, i : i + 1])
-            nc.scalar.activation(out=junk[1][:], in_=tb[i][:], func=ACT.Square, bias=eps_t[:], accum_out=sums2[:, i : i + 1])
+            nc.scalar.activation(out=junk[0][:], in_=srow[i][:], func=ACT.Ln, bias=eps_t[:], scale=-1.0, accum_out=sumln[:, i : i + 1])
+            nc.scalar.activation(out=junk[1][:], in_=srow[i][:], func=ACT.Square, bias=eps_t[:], scale=-1.0, accum_out=sums2[:, i : i + 1])
 
         def kl_mu_sum(i):
             nc.scalar.activation(out=junk[2][:], in_=mu[i][:], func=ACT.Square, accum_out=summu[:, i : i + 1])
 
         def scale_noise(i):
+            sn[i] = snp.tile([P, D], F32, name="sn")
             nc.vector.scalar_tensor_tensor(
-                out=ta[i][:], in0=tb[i][:], scalar=SCALE_EPS, in1=nch[i // CH][:, i % CH, :], op0=ALU.add, op1=ALU.mult
+                out=sn[i][:], in0=srow[i][:], scalar=-SCALE_EPS, in1=nch[i // G][:, i % G, :], op0=ALU.add, op1=ALU.mult
             )
 
         def sample(i):
-            nc.gpsimd.tensor_tensor(out=ta[i][:], in0=ta[i][:], in1=mu[i][:], op=ALU.add)
-            nc.sync.dma_start(out=z_v[:, i, :], in_=ta[i][:])
+            if i % 2 == 0:
+                zt[i // 2] = grp.tile([P, 2, D], F32, name="zt")
+            nc.gpsimd.tensor_tensor(out=zt[i // 2][:, i % 2, :], in0=mu[i][:], in1=sn[i][:], op=ALU.subtract)
 
-        def tr_z(i):
-            zps[i] = ps_t.tile([P, 4, P], F32, name="zps", tag="tr")
-            for t in range(4):
-                nc.tensor.transpose(zps[i][:, t, :], ta[i][:, t * P : (t + 1) * P], ident[:])
+        def round_z(j):
+            nc.sync.dma_start(out=z_v[:, 2 * j : 2 * j + 2, :], in_=zt[j][:])
+            zb[j] = grp.tile([P, 2, D], BF16, name="zb", align_bytes=64)
+            nc.gpsimd.tensor_scalar(out=zb[j][:], in0=zt[j][:], scalar1=1.0, scalar2=0.0, op0=ALU.mult, op1=ALU.add)
 
-        def ev_z(i):
-            zg[i] = grp.tile([P, P, 4], BF16, name="zg", align_bytes=64)
-            if i % EVZ_MOD == 0:
-                nc.vector.tensor_copy(out=zg[i][:], in_=zps[i][:].rearrange("p t r -> p r t"))
-            else:
-                nc.scalar.copy(out=zg[i][:], in_=zps[i][:].rearrange("p t r -> p r t"))
+        def tr_z(j):
+            zps[j] = ps_1.tile([P, 4, P], F32, name="zps", tag="z")
+            for jj in range(2):
+                tr_words(zps[j][:, 2 * jj : 2 * jj + 2, :], zb[j][:, jj, :])
 
-        EVZ_MOD = 2
+        def ev_z(j):
+            zg[j] = grp.tile([P, 2, P, 2], F32, name="zg", align_bytes=64)
+            nc.scalar.copy(out=zg[j][:], in_=zps[j][:].rearrange("p (j u) r -> p j r u", u=2))
 
-        def q_z(i):
-            zc[i] = grp.tile([P, P], U32, name="zc", align_bytes=64)
-            zs[i] = grp.tile([P, P], U8, name="zs", align_bytes=64)
-            nc.vector.quantize_mx(out=zc[i][:].bitcast(FP8X4), scales=zs[i][:], in_=zg[i][:].rearrange("p r t -> p (r t)"))
+        def q_z(j):
+            zc[j] = grp.tile([P, 2 * P], U32, name="zc", align_bytes=64)
+            zs[j] = grp.tile([P, 2 * P], U8, name="zs", align_bytes=64)
+            nc.vector.quantize_mx(
+                out=zc[j][:].bitcast(FP8X4), scales=zs[j][:], in_=zg[j][:].rearrange("p j r u -> p (j r u)").bitcast(BF16)
+            )
 
         def mm2(i):
-            pps[i] = ps_m.tile([P, D], F32, name="acc", tag="m2")
-            nc.tensor.matmul_mx(
-                out=pps[i][:],
-                lhsT=zc[i][:].bitcast(FP8X4),
-                lhsT_scale=zs[i][:],
-                rhs=w2c[:].bitcast(FP8X4),
-                rhs_scale=w2s[:],
-                start=True,
-                stop=True,
-            )
+            pps[i] = ps_1.tile([P, D], F32, name="acc2", tag="mm2")
+            cols = slice((i % 2) * P, (i % 2 + 1) * P)
+            mx(pps[i][:], zc[i // 2][:, cols], zs[i // 2][:, cols], w2c[:], w2s[:])
+
+        NEG = 4
+        have_mean = set()
 
         def pre_add(i):
             nc.vector.scalar_tensor_tensor(
-                out=tb[i][:], in0=pps[i][:], scalar=0.0, in1=b_dec[:], op0=ALU.add, op1=ALU.add, accum_out=sumpre[:, i : i + 1]
+                out=xrow(i), in0=pps[i][:], scalar=0.0, in1=b_dec[:], op0=ALU.add, op1=ALU.add, accum_out=sumpre[:, i : i + 1]
             )
             if i % NEG == NEG - 1:
                 cols = slice(i + 1 - NEG, i + 1)
                 nc.scalar.mul(out=negmean[:, cols], in_=sumpre[:, cols], mul=-1.0 / D)
-
-        NEG = 8
+                for t in range(i + 1 - NEG, i + 1):
+                    have_mean.add(t)
 
         def sq_dev(i):
+            assert i in have_mean
             nc.scalar.activation(
-                out=junk[i % 4][:], in_=tb[i][:], func=ACT.Square, bias=negmean[:, i : i + 1], accum_out=sumdev[:, i : i + 1]
+                out=junk[i % 4][:], in_=xrow(i), func=ACT.Square, bias=negmean[:, i : i + 1], accum_out=sumdev[:, i : i + 1]
             )
-            if i % CH == CH - 1:
-                cols = slice(i + 1 - CH, i + 1)
+            if i % G == G - 1:
+                cols = slice(i + 1 - G, i + 1)
                 nc.gpsimd.tensor_scalar(
                     out=varep[:, cols], in0=sumdev[:, cols], scalar1=1.0 / D, scalar2=LN_EPS, op0=ALU.mult, op1=ALU.add
                 )
@@ -319,21 +341,20 @@ def tile_latentvaeblock_pa_t_kernel(
 
         def centre(i):
             nc.vector.scalar_tensor_tensor(
-                out=tb[i][:], in0=tb[i][:], scalar=negmean[:, i : i + 1], in1=g_ps[:], op0=ALU.add, op1=ALU.mult
+                out=xrow(i), in0=xrow(i), scalar=negmean[:, i : i + 1], in1=g_row[:], op0=ALU.add, op1=ALU.mult
             )
 
         def affine(i):
             nc.vector.scalar_tensor_tensor(
-                out=tb[i][:], in0=tb[i][:], scalar=rstd[:, i : i + 1], in1=b_ps[:], op0=ALU.mult, op1=ALU.add
+                out=xrow(i), in0=xrow(i), scalar=rstd[:, i : i + 1], in1=b_row[:], op0=ALU.mult, op1=ALU.add
             )
 
         def silu_store(i):
-            nc.scalar.activation(out=tb[i][:], in_=tb[i][:], func=ACT.Silu)
-            nc.sync.dma_start(out=d_v[:, i, :], in_=tb[i][:])
+            nc.scalar.activation(out=pair(i), in_=pair(i), func=ACT.Silu)
+            nc.sync.dma_start(out=d_v[:, i : i + 2, :], in_=et[i // G][:, i % G : i % G + 2, :])
 
         LEAD_SQ = 8
         LEAD_C = 6
-        EARLY = 3
 
         def on(i):
             return 0 <= i < NT
@@ -345,48 +366,63 @@ def tile_latentvaeblock_pa_t_kernel(
                 centre(n - (LEAD_SQ - LEAD_C))
             if on(n - LEAD_SQ):
                 affine(n - LEAD_SQ)
-            if on(n - LEAD_SQ - 1):
-                silu_store(n - LEAD_SQ - 1)
+            m = n - LEAD_SQ - 2
+            if on(m) and m % 2 == 0:
+                silu_store(m)
 
-        mps[0] = mm1(0, 0, "m1")
-        mps[1] = mm1(1, 0, "m1")
-        ln1(0)
+        steps = [0]
+
+        def run_steps(count):
+            for q in range(count):
+                step3(steps[0])
+                steps[0] += 1
+
+        FILL = 7
         DRAIN = 5
-        for k in range(NT + DRAIN):
-            if on(k - 2):
-                tr_z(k - 2)
-            if on(k - 4):
-                mm2(k - 4)
+        MU = 6
+        for k in range(-FILL, NT + DRAIN):
             if on(k + 1):
-                ln1(k + 1)
-            if on(k - 1):
-                kl_scale_sums(k - 1)
-                kl_mu_sum(k - 1)
+                tr_s(k + 1)
+            if on(k + 5):
+                mm_lv(k + 5, ps_lv, "lv")
+            if on(k + MU):
+                mm_mu(k + MU)
+            if on(k - 5):
+                mm2(k - 5)
+            if k % 2 == 1 and on(k - 3):
+                tr_z((k - 3) // 2)
             if on(k):
-                softplus_guard(k)
-            if on(k - 3):
-                q_z(k - 3)
+                kl_scale_sums(k)
+            if k % 2 == 0 and on(k - 4):
+                ev_z((k - 4) // 2)
+            if k % 2 == 1 and on(k + 7):
+                ln1(k + 7)
             if on(k - 1):
                 scale_noise(k - 1)
+            if on(k + 5):
+                guard(k + 5)
+            if on(k - 1):
                 sample(k - 1)
-            if k % CH == 1 and k // CH + 2 < NCH:
-                load_n(k // CH + 2)
-            if on(k):
-                mu_add(k)
-            if on(k + 2):
-                mps[k + 2] = mm1(k + 2, 0, "m1")
+                if k % 2 == 0:
+                    round_z((k - 2) // 2)
+            if k % G == 1 and 2 <= k // G + 2 < NG:
+                load_n(k // G + 2)
+            if k % 2 == 0 and on(k - 4):
+                q_z((k - 4) // 2)
+            if on(k + MU):
+                mu_add(k + MU)
+            if on(k + MU - 1):
+                kl_mu_sum(k + MU - 1)
             if on(k - 5):
                 pre_add(k - 5)
-            if on(k - 2):
-                ev_z(k - 2)
             if k >= NT:
-                for n in range(EARLY * (k - NT), EARLY * (k - NT + 1)):
-                    step3(n)
+                run_steps(3)
+            elif k >= 25:
+                run_steps(1)
 
         nc.gpsimd.tensor_tensor(out=kl_a[:], in0=sums2[:], in1=summu[:], op=ALU.add)
         nc.gpsimd.tensor_scalar(out=kl_b[:], in0=kl_a[:], scalar1=0.5, scalar2=-0.5 * D, op0=ALU.mult, op1=ALU.add)
         nc.gpsimd.tensor_tensor(out=kl_c[:], in0=kl_b[:], in1=sumln[:], op=ALU.subtract)
         nc.sync.dma_start(out=kl_v, in_=kl_c[:])
 
-        for n in range(DRAIN * EARLY, NT + LEAD_SQ + 1):
-            step3(n)
+        run_steps(NT + LEAD_SQ + 2 - steps[0])

@@ -46,7 +46,8 @@ def tile_latentvaeblock_pa_t_kernel(
         mup = ctx.enter_context(tc.tile_pool(name="mup", bufs=10))
         snp = ctx.enter_context(tc.tile_pool(name="snp", bufs=3))
         ps_lv = ctx.enter_context(tc.psum_pool(name="ps_lv", bufs=2))
-        ps_sr = ctx.enter_context(tc.psum_pool(name="ps_sr", bufs=3))
+        ps_sr = ctx.enter_context(tc.psum_pool(name="ps_sr", bufs=2))
+        ps_mu = ctx.enter_context(tc.psum_pool(name="ps_mu", bufs=2))
         ps_1 = ctx.enter_context(tc.psum_pool(name="ps_1", bufs=1))
 
         ident = const.tile([P, P], F32, name="ident")
@@ -194,7 +195,7 @@ def tile_latentvaeblock_pa_t_kernel(
         ev_h(1)
         q_h(0)
         tr_h(3)
-        bps = ps_1.tile([P, P], BF16, name="bps", tag="mu")
+        bps = ps_mu.tile([P, P], BF16, name="bps", tag="mu")
         nc.tensor.transpose(bps[:], vecs[:], identb[:])
         nc.vector.tensor_scalar(out=bcol[:], in0=bps[:, 0:G], scalar1=-1.0, scalar2=None, op0=ALU.mult)
         q_h(1)
@@ -255,16 +256,20 @@ def tile_latentvaeblock_pa_t_kernel(
             )
 
         def tr_s(i):
-            srow[i] = ps_sr.tile([P, D], F32, name="srow", tag="sr")
             for n in range(G):
                 nc.tensor.transpose(
                     srow[i][:, n * P : (n + 1) * P], et[i // G][:, n, (i % G) * P : (i % G + 1) * P], ident[:]
                 )
 
         def mm_mu(i):
-            mup_ps[i] = ps_1.tile([P, D], F32, name="accmu", tag="mu")
+            mup_ps[i] = ps_mu.tile([P, D], F32, name="accmu", tag="mu")
             cols = slice(i * P, (i + 1) * P)
             mx(mup_ps[i][:], hc[:, cols], hs[:, cols], w1c[:, 0:D], w1s[:, 0:D])
+
+        def warm_up(i):
+            srow[i] = ps_sr.tile([P, D], F32, name="srow", tag="sr")
+            cols = slice(i * P, (i + 1) * P)
+            mx(srow[i][:], hc[:, cols], hs[:, cols], w1c[:, 0:D], w1s[:, 0:D])
 
         def mu_add(i):
             mu[i] = mup.tile([P, D], F32, name="mu")
@@ -377,28 +382,29 @@ def tile_latentvaeblock_pa_t_kernel(
                 step3(steps[0])
                 steps[0] += 1
 
-        FILL = 7
-        DRAIN = 5
+        FILL = 8
+        DRAIN = 7
         MU = 6
+        mm_mu(0)
         for k in range(-FILL, NT + DRAIN):
+            if on(k - 7):
+                mm2(k - 7)
+            if on(k + 6):
+                mm_lv(k + 6, ps_lv, "lv")
+            if on(k + MU + 1) and k + MU + 1 > 0:
+                mm_mu(k + MU + 1)
+            if on(k + 1):
+                warm_up(k + 1)
+            if k % 2 == 0 and on(k - 4):
+                tr_z((k - 4) // 2)
             if on(k + 1):
                 tr_s(k + 1)
-            if on(k + 5):
-                mm_lv(k + 5, ps_lv, "lv")
-            if on(k + MU):
-                mm_mu(k + MU)
-            if on(k - 5):
-                mm2(k - 5)
-            if k % 2 == 1 and on(k - 3):
-                tr_z((k - 3) // 2)
             if on(k):
                 kl_scale_sums(k)
-            if k % 2 == 0 and on(k - 4):
-                ev_z((k - 4) // 2)
-            if k % 2 == 1 and on(k + 7):
-                ln1(k + 7)
-            if on(k - 1):
-                scale_noise(k - 1)
+            if k % 2 == 0 and on(k + 8):
+                ln1(k + 8)
+            if k % 2 == 1 and on(k - 5):
+                ev_z((k - 5) // 2)
             if on(k + 5):
                 guard(k + 5)
             if on(k - 1):
@@ -407,14 +413,16 @@ def tile_latentvaeblock_pa_t_kernel(
                     round_z((k - 2) // 2)
             if k % G == 1 and 2 <= k // G + 2 < NG:
                 load_n(k // G + 2)
-            if k % 2 == 0 and on(k - 4):
-                q_z((k - 4) // 2)
             if on(k + MU):
                 mu_add(k + MU)
+            if k % 2 == 0 and on(k - 6):
+                q_z((k - 6) // 2)
+            if on(k - 7):
+                pre_add(k - 7)
+            if on(k):
+                scale_noise(k)
             if on(k + MU - 1):
                 kl_mu_sum(k + MU - 1)
-            if on(k - 5):
-                pre_add(k - 5)
             if k >= NT:
                 run_steps(3)
             elif k >= 25:

@@ -1,3 +1,4 @@
+import math
 from contextlib import ExitStack
 
 import concourse.mybir as mybir
@@ -55,14 +56,12 @@ def tile_latentvaeblock_pa_t_kernel(
         identb = const.tile([P, P], BF16, name="identb")
         vecs = const.tile([P, P], BF16, name="vecs")
         one_t = const.tile([P, 1], F32, name="one_t")
-        eps_t = const.tile([P, 1], F32, name="eps_t")
         warm = const.tile([P, 1], F32, name="warm")
         floor_t = const.tile([P, 1], F32, name="floor_t")
         mhalf = const.tile([P, G], F32, name="mhalf")
         nc.vector.memset(one_t[:], 1.0)
         nc.vector.memset(floor_t[:], SIG_FLOOR)
         nc.vector.memset(vecs[:], 0.0)
-        nc.vector.memset(eps_t[:], SCALE_EPS)
         nc.vector.memset(mhalf[:], -0.5)
         nc.scalar.dma_start(out=vecs[0:G, :], in_=enc_b_out[D : 2 * D].rearrange("(n p) -> n p", p=P))
         nc.scalar.activation(out=warm[:], in_=one_t[:], func=ACT.Sigmoid)
@@ -73,6 +72,7 @@ def tile_latentvaeblock_pa_t_kernel(
         g_row = const.tile([P, D], BF16, name="g_row")
         b_row = const.tile([P, D], BF16, name="b_row")
         bcol = const.tile([P, G], F32, name="bcol")
+        bcol2 = const.tile([P, G], F32, name="bcol2")
         w1c = const.tile([P, 2 * D], U32, name="w1c", align_bytes=64)
         w1s = const.tile([P, 2 * D], U8, name="w1s", align_bytes=64)
         w2c = const.tile([P, D], U32, name="w2c", align_bytes=64)
@@ -198,6 +198,7 @@ def tile_latentvaeblock_pa_t_kernel(
         bps = ps_mu.tile([P, P], BF16, name="bps", tag="mu")
         nc.tensor.transpose(bps[:], vecs[:], identb[:])
         nc.vector.tensor_scalar(out=bcol[:], in0=bps[:, 0:G], scalar1=-1.0, scalar2=None, op0=ALU.mult)
+        nc.vector.tensor_scalar(out=bcol2[:], in0=bps[:, 0:G], scalar1=-1.0, scalar2=-SCALE_EPS, op0=ALU.mult, op1=ALU.add)
         q_h(1)
         mm_lv(0, ps_lv, "lv")
         mm_lv(1, ps_lv, "lv")
@@ -246,13 +247,13 @@ def tile_latentvaeblock_pa_t_kernel(
         pps = {}
 
         def ln1(u):
-            nc.scalar.activation(out=pair(u), in_=pair(u), func=ACT.Ln, bias=floor_t[:])
+            nc.scalar.activation(out=pair(u), in_=pair(u), func=ACT.Ln, bias=floor_t[:], scale=math.exp(-SCALE_EPS))
 
         def guard(u):
             n = u % G
             dst = et[u // G][:, n, :]
             nc.vector.scalar_tensor_tensor(
-                out=dst, in0=lvp[u][:], scalar=bcol[:, n : n + 1], in1=dst, op0=ALU.add, op1=ALU.min
+                out=dst, in0=lvp[u][:], scalar=bcol2[:, n : n + 1], in1=dst, op0=ALU.add, op1=ALU.min
             )
 
         def tr_s(i):
@@ -273,20 +274,18 @@ def tile_latentvaeblock_pa_t_kernel(
 
         def mu_add(i):
             mu[i] = mup.tile([P, D], F32, name="mu")
-            nc.vector.tensor_tensor(out=mu[i][:], in0=mup_ps[i][:], in1=b_mu[:], op=ALU.add)
+            nc.vector.tensor_tensor(out=mu[i][:], in0=b_mu[:], in1=mup_ps[i][:], op=ALU.add)
 
         def kl_scale_sums(i):
-            nc.scalar.activation(out=junk[0][:], in_=srow[i][:], func=ACT.Ln, bias=eps_t[:], scale=-1.0, accum_out=sumln[:, i : i + 1])
-            nc.scalar.activation(out=junk[1][:], in_=srow[i][:], func=ACT.Square, bias=eps_t[:], scale=-1.0, accum_out=sums2[:, i : i + 1])
+            nc.scalar.activation(out=junk[0][:], in_=srow[i][:], func=ACT.Ln, scale=-1.0, accum_out=sumln[:, i : i + 1])
+            nc.scalar.activation(out=junk[1][:], in_=srow[i][:], func=ACT.Square, accum_out=sums2[:, i : i + 1])
 
         def kl_mu_sum(i):
             nc.scalar.activation(out=junk[2][:], in_=mu[i][:], func=ACT.Square, accum_out=summu[:, i : i + 1])
 
         def scale_noise(i):
             sn[i] = snp.tile([P, D], F32, name="sn")
-            nc.vector.scalar_tensor_tensor(
-                out=sn[i][:], in0=srow[i][:], scalar=-SCALE_EPS, in1=nch[i // G][:, i % G, :], op0=ALU.add, op1=ALU.mult
-            )
+            nc.vector.tensor_tensor(out=sn[i][:], in0=nch[i // G][:, i % G, :], in1=srow[i][:], op=ALU.mult)
 
         def sample(i):
             if i % 2 == 0:
@@ -324,7 +323,7 @@ def tile_latentvaeblock_pa_t_kernel(
 
         def pre_add(i):
             nc.vector.scalar_tensor_tensor(
-                out=xrow(i), in0=pps[i][:], scalar=0.0, in1=b_dec[:], op0=ALU.add, op1=ALU.add, accum_out=sumpre[:, i : i + 1]
+                out=xrow(i), in0=b_dec[:], scalar=0.0, in1=pps[i][:], op0=ALU.add, op1=ALU.add, accum_out=sumpre[:, i : i + 1]
             )
             if i % NEG == NEG - 1:
                 cols = slice(i + 1 - NEG, i + 1)

@@ -44,11 +44,10 @@ def tile_latentvaeblock_pa_t_kernel(
         hst = ctx.enter_context(tc.tile_pool(name="hst", bufs=4))
         nst = ctx.enter_context(tc.tile_pool(name="nst", bufs=3))
         grp = ctx.enter_context(tc.tile_pool(name="grp", bufs=3))
-        mup = ctx.enter_context(tc.tile_pool(name="mup", bufs=10))
+        mup = ctx.enter_context(tc.tile_pool(name="mup", bufs=20))
         snp = ctx.enter_context(tc.tile_pool(name="snp", bufs=3))
         ps_lv = ctx.enter_context(tc.psum_pool(name="ps_lv", bufs=2))
-        ps_sr = ctx.enter_context(tc.psum_pool(name="ps_sr", bufs=2))
-        ps_mu = ctx.enter_context(tc.psum_pool(name="ps_mu", bufs=2))
+        ps_sr = ctx.enter_context(tc.psum_pool(name="ps_sr", bufs=3))
         ps_1 = ctx.enter_context(tc.psum_pool(name="ps_1", bufs=1))
 
         ident = const.tile([P, P], F32, name="ident")
@@ -71,6 +70,12 @@ def tile_latentvaeblock_pa_t_kernel(
         b_dec = const.tile([P, D], BF16, name="b_dec")
         g_row = const.tile([P, D], BF16, name="g_row")
         b_row = const.tile([P, D], BF16, name="b_row")
+        b_all = const.tile([P, D], BF16, name="b_all")
+        g_all = const.tile([P, D], BF16, name="g_all")
+        ones = const.tile([P, P], BF16, name="ones")
+        nc.gpsimd.memset(g_row[:], 0.0)
+        nc.gpsimd.memset(b_row[:], 0.0)
+        nc.gpsimd.memset(ones[:], 1.0)
         bcol = const.tile([P, G], F32, name="bcol")
         bcol2 = const.tile([P, G], F32, name="bcol2")
         w1c = const.tile([P, 2 * D], U32, name="w1c", align_bytes=64)
@@ -129,14 +134,21 @@ def tile_latentvaeblock_pa_t_kernel(
                 nc.tensor.transpose(dst[:, u, :], rows.bitcast(F32)[:, u * P : (u + 1) * P], ident[:])
 
         def tr_h(j):
-            hps[j] = ps_1.tile([P, 4, P], F32, name="hps", tag="z" if j % 2 == 0 else "mm2")
+            if j == 3:
+                hps[j] = ps_sr.tile([P, 4, P], F32, name="hps", tag="sr")
+            else:
+                hps[j] = ps_1.tile([P, 4, P], F32, name="hps", tag=("mu", "z", "mm2")[j % 3])
             for jj in range(2):
                 i = 2 * j + jj
                 tr_words(hps[j][:, 2 * jj : 2 * jj + 2, :], hch[i // G][:, i % G, :])
 
         def ev_h(j):
             hg[j] = grp.tile([P, 2, P, 2], F32, name="hg", align_bytes=64)
-            nc.vector.tensor_copy(out=hg[j][:], in_=hps[j][:].rearrange("p (j u) r -> p j r u", u=2))
+            src = hps[j][:].rearrange("p (j u) r -> p j r u", u=2)
+            if j < 2:
+                nc.scalar.copy(out=hg[j][:], in_=src)
+            else:
+                nc.vector.tensor_copy(out=hg[j][:], in_=src)
 
         def q_h(j):
             cols = slice(2 * j * P, (2 * j + 2) * P)
@@ -149,8 +161,11 @@ def tile_latentvaeblock_pa_t_kernel(
                 out=out, lhsT=lc.bitcast(FP8X4), lhsT_scale=ls, rhs=rc.bitcast(FP8X4), rhs_scale=rs, start=True, stop=True
             )
 
-        def mm_lv(u, pool, tag):
-            lvp[u] = pool.tile([P, D], F32, name="acc", tag=tag)
+        def mm_lv(u, wide=False):
+            if wide and u % G >= 2:
+                lvp[u] = ps_sr.tile([P, D], F32, name="acc", tag="sr")
+            else:
+                lvp[u] = ps_lv.tile([P, D], F32, name="acc", tag="lv")
             wcols = slice(D + (u % G) * P, D + (u % G + 1) * P)
             rows = slice((u // G) * G * P, (u // G + 1) * G * P)
             mx(lvp[u][:], w1c[:, wcols], w1s[:, wcols], hc[:, rows], hs[:, rows])
@@ -162,18 +177,39 @@ def tile_latentvaeblock_pa_t_kernel(
         def pair(u):
             return et[u // G][:, u % G : u % G + 2, :].rearrange("p a c -> p (a c)")
 
-        def regroup_w(which):
-            wg = wst.tile([P, D, 4], BF16, name="wg", tag="w", align_bytes=64)
-            dst = wg[:].rearrange("p (c i) t -> p c t i", i=4)
-            src = wraw[which][:].rearrange("p t (c i) -> p c t i", i=4)
+        wgs = {}
+
+        def regroup_w(which, half):
+            if half == 0:
+                wgs[which] = wst.tile([P, D, 4], BF16, name="wg", tag="w", align_bytes=64)
+            cols = slice(half * D // 2, (half + 1) * D // 2)
+            dst = wgs[which][:, cols, :].rearrange("p (c i) t -> p c t i", i=4)
+            src = wraw[which][:, :, cols].rearrange("p t (c i) -> p c t i", i=4)
             if which == "lv":
                 nc.vector.tensor_scalar(out=dst, in0=src, scalar1=-1.0, scalar2=None, op0=ALU.mult)
             else:
                 nc.vector.tensor_copy(out=dst, in_=src)
-            return wg
 
         def quant_w(wg, codes, scales):
             nc.vector.quantize_mx(out=codes.bitcast(FP8X4), scales=scales, in_=wg[:].rearrange("p c t -> p (c t)"))
+
+        mup_ps = {}
+        mu = {}
+        mus = [0]
+
+        def mm_mu(i):
+            mup_ps[i] = ps_1.tile([P, D], F32, name="accmu", tag=("mu", "z", "mm2")[i % 3] if i < 8 else "mu")
+            cols = slice(i * P, (i + 1) * P)
+            mx(mup_ps[i][:], hc[:, cols], hs[:, cols], w1c[:, 0:D], w1s[:, 0:D])
+
+        def mu_add(i):
+            mu[i] = mup.tile([P, D], F32, name="mu")
+            nc.vector.tensor_tensor(out=mu[i][:], in0=b_mu[:], in1=mup_ps[i][:], op=ALU.add)
+
+        def next_mu():
+            if mus[0] < NT:
+                mu_add(mus[0])
+                mus[0] += 1
 
         load_w("lv", enc_w_out[:, D : 2 * D])
         load_h(0, parts=2)
@@ -184,58 +220,63 @@ def tile_latentvaeblock_pa_t_kernel(
         load_w("dec", dec_w_in)
         nc.sync.dma_start(out=b_mu[:], in_=enc_b_out[0:D].partition_broadcast(P))
         nc.sync.dma_start(out=b_dec[:], in_=dec_b_in.partition_broadcast(P))
-        nc.sync.dma_start(out=g_row[:], in_=dec_ln_g.partition_broadcast(P))
-        nc.sync.dma_start(out=b_row[:], in_=dec_ln_b.partition_broadcast(P))
-        wg_lv = regroup_w("lv")
+        nc.sync.dma_start(out=b_all[:], in_=dec_ln_b.partition_broadcast(P))
+        nc.sync.dma_start(out=g_all[:], in_=dec_ln_g.partition_broadcast(P))
+        nc.sync.dma_start(out=g_row[0:1, :], in_=dec_ln_g.rearrange("(o n) -> o n", o=1))
+        nc.sync.dma_start(out=b_row[0:1, :], in_=dec_ln_b.rearrange("(o n) -> o n", o=1))
         tr_h(0)
         tr_h(1)
-        quant_w(wg_lv, w1c[:, D : 2 * D], w1s[:, D : 2 * D])
-        ev_h(0)
-        tr_h(2)
-        ev_h(1)
-        q_h(0)
-        tr_h(3)
-        bps = ps_mu.tile([P, P], BF16, name="bps", tag="mu")
+        bps = ps_sr.tile([P, P], BF16, name="bps", tag="sr")
         nc.tensor.transpose(bps[:], vecs[:], identb[:])
+        tr_h(2)
+        tr_h(3)
+        regroup_w("lv", 0)
+        regroup_w("lv", 1)
+        ev_h(0)
+        ev_h(1)
+        quant_w(wgs["lv"], w1c[:, D : 2 * D], w1s[:, D : 2 * D])
+        q_h(0)
         nc.vector.tensor_scalar(out=bcol[:], in0=bps[:, 0:G], scalar1=-1.0, scalar2=None, op0=ALU.mult)
         nc.vector.tensor_scalar(out=bcol2[:], in0=bps[:, 0:G], scalar1=-1.0, scalar2=-SCALE_EPS, op0=ALU.mult, op1=ALU.add)
         q_h(1)
-        mm_lv(0, ps_lv, "lv")
-        mm_lv(1, ps_lv, "lv")
+        for u in range(G):
+            mm_lv(u, wide=True)
         ev_h(2)
+        ev_h(3)
+        q_h(2)
+        q_h(3)
         load_h(4)
-        for j in range(NP):
-            if j + 4 < NP:
-                tr_h(j + 4)
-                if j % 2 == 0 and j // 2 + 5 < NG:
-                    load_h(j // 2 + 5)
-            if j + 3 < NP:
-                ev_h(j + 3)
-            if j + 2 < NP:
-                q_h(j + 2)
-            if j + 1 < NP:
-                for u in (2 * j + 2, 2 * j + 3):
-                    if j % 2 == 1:
-                        mm_lv(u, ps_lv, "lv")
-                    else:
-                        mm_lv(u, ps_sr, "sr")
-            exp_lv(2 * j)
-            exp_lv(2 * j + 1)
-            if j == 3:
-                wg_mu = regroup_w("mu")
-            if j == 5:
-                quant_w(wg_mu, w1c[:, 0:D], w1s[:, 0:D])
-            if j == 7:
-                wg_w2 = regroup_w("dec")
-            if j == 9:
-                quant_w(wg_w2, w2c[:], w2s[:])
-            if j == 10:
+        for g in range(NG):
+            if g + 2 < NG:
+                tr_h(2 * g + 4)
+                tr_h(2 * g + 5)
+                if g + 5 < NG:
+                    load_h(g + 5)
+            if g + 2 < NG:
+                ev_h(2 * g + 4)
+                ev_h(2 * g + 5)
+                q_h(2 * g + 4)
+                q_h(2 * g + 5)
+            if g < 2:
+                regroup_w("mu", g)
+            elif g < 4:
+                regroup_w("dec", g - 2)
+            if g == 2:
+                quant_w(wgs["mu"], w1c[:, 0:D], w1s[:, 0:D])
+            if g == 4:
+                quant_w(wgs["dec"], w2c[:], w2s[:])
+            for n in range(G):
+                exp_lv(G * g + n)
+                if g + 1 < NG:
+                    mm_lv(G * (g + 1) + n, wide=True)
+                if g >= NG - 2:
+                    mm_mu(mus[0])
+                    next_mu()
+            if g == 5:
                 load_n(0)
-            if j == 12:
+            if g == 6:
                 load_n(1)
 
-        mup_ps = {}
-        mu = {}
         srow = {}
         sn = {}
         zt = {}
@@ -257,24 +298,11 @@ def tile_latentvaeblock_pa_t_kernel(
             )
 
         def tr_s(i):
+            srow[i] = ps_sr.tile([P, D], F32, name="srow", tag="sr")
             for n in range(G):
                 nc.tensor.transpose(
                     srow[i][:, n * P : (n + 1) * P], et[i // G][:, n, (i % G) * P : (i % G + 1) * P], ident[:]
                 )
-
-        def mm_mu(i):
-            mup_ps[i] = ps_mu.tile([P, D], F32, name="accmu", tag="mu")
-            cols = slice(i * P, (i + 1) * P)
-            mx(mup_ps[i][:], hc[:, cols], hs[:, cols], w1c[:, 0:D], w1s[:, 0:D])
-
-        def warm_up(i):
-            srow[i] = ps_sr.tile([P, D], F32, name="srow", tag="sr")
-            cols = slice(i * P, (i + 1) * P)
-            mx(srow[i][:], hc[:, cols], hs[:, cols], w1c[:, 0:D], w1s[:, 0:D])
-
-        def mu_add(i):
-            mu[i] = mup.tile([P, D], F32, name="mu")
-            nc.vector.tensor_tensor(out=mu[i][:], in0=b_mu[:], in1=mup_ps[i][:], op=ALU.add)
 
         def kl_scale_sums(i):
             nc.scalar.activation(out=junk[0][:], in_=srow[i][:], func=ACT.Ln, scale=-1.0, accum_out=sumln[:, i : i + 1])
@@ -304,7 +332,11 @@ def tile_latentvaeblock_pa_t_kernel(
 
         def ev_z(j):
             zg[j] = grp.tile([P, 2, P, 2], F32, name="zg", align_bytes=64)
-            nc.scalar.copy(out=zg[j][:], in_=zps[j][:].rearrange("p (j u) r -> p j r u", u=2))
+            src = zps[j][:].rearrange("p (j u) r -> p j r u", u=2)
+            if j % 3 == 0:
+                nc.scalar.copy(out=zg[j][:], in_=src)
+            else:
+                nc.vector.tensor_copy(out=zg[j][:], in_=src)
 
         def q_z(j):
             zc[j] = grp.tile([P, 2 * P], U32, name="zc", align_bytes=64)
@@ -314,7 +346,8 @@ def tile_latentvaeblock_pa_t_kernel(
             )
 
         def mm2(i):
-            pps[i] = ps_1.tile([P, D], F32, name="acc2", tag="mm2")
+            late = i >= 17 and i % 2 == 1
+            pps[i] = ps_1.tile([P, D], F32, name="acc2", tag="mu" if late else "mm2")
             cols = slice((i % 2) * P, (i % 2 + 1) * P)
             mx(pps[i][:], zc[i // 2][:, cols], zs[i // 2][:, cols], w2c[:], w2s[:])
 
@@ -325,17 +358,28 @@ def tile_latentvaeblock_pa_t_kernel(
             nc.vector.scalar_tensor_tensor(
                 out=xrow(i), in0=b_dec[:], scalar=0.0, in1=pps[i][:], op0=ALU.add, op1=ALU.add, accum_out=sumpre[:, i : i + 1]
             )
+
+        def mean(i):
             if i % NEG == NEG - 1:
                 cols = slice(i + 1 - NEG, i + 1)
-                nc.scalar.mul(out=negmean[:, cols], in_=sumpre[:, cols], mul=-1.0 / D)
+                nc.vector.tensor_scalar(out=negmean[:, cols], in0=sumpre[:, cols], scalar1=-1.0 / D, scalar2=None, op0=ALU.mult)
                 for t in range(i + 1 - NEG, i + 1):
                     have_mean.add(t)
 
-        def sq_dev(i):
+        gb_ps = {}
+
+        def spread_gb():
+            for name, row in (("g", g_row), ("b", b_row)):
+                gb_ps[name] = ps_lv.tile([P, D], F32, name="gb_ps", tag="lv")
+                nc.tensor.matmul(out=gb_ps[name][:], lhsT=ones[:], rhs=row[:], start=True, stop=True)
+
+        def deviations(i):
             assert i in have_mean
             nc.scalar.activation(
                 out=junk[i % 4][:], in_=xrow(i), func=ACT.Square, bias=negmean[:, i : i + 1], accum_out=sumdev[:, i : i + 1]
             )
+
+        def group_rstd(i):
             if i % G == G - 1:
                 cols = slice(i + 1 - G, i + 1)
                 nc.gpsimd.tensor_scalar(
@@ -345,32 +389,41 @@ def tile_latentvaeblock_pa_t_kernel(
 
         def centre(i):
             nc.vector.scalar_tensor_tensor(
-                out=xrow(i), in0=xrow(i), scalar=negmean[:, i : i + 1], in1=g_row[:], op0=ALU.add, op1=ALU.mult
+                out=xrow(i), in0=xrow(i), scalar=negmean[:, i : i + 1], in1=gb_ps.get("g", g_all)[:], op0=ALU.add, op1=ALU.mult
             )
 
         def affine(i):
-            nc.vector.scalar_tensor_tensor(
-                out=xrow(i), in0=xrow(i), scalar=rstd[:, i : i + 1], in1=b_row[:], op0=ALU.mult, op1=ALU.add
-            )
+            if i % 4 == 1:
+                nc.gpsimd.tensor_scalar(
+                    out=xrow(i), in0=xrow(i), scalar1=rstd[:, i : i + 1], scalar2=0.0, op0=ALU.mult, op1=ALU.add
+                )
+                nc.gpsimd.tensor_tensor(out=xrow(i), in0=xrow(i), in1=b_all[:], op=ALU.add)
+            else:
+                nc.vector.scalar_tensor_tensor(
+                    out=xrow(i), in0=xrow(i), scalar=rstd[:, i : i + 1], in1=gb_ps["b"][:], op0=ALU.mult, op1=ALU.add
+                )
 
         def silu_store(i):
             nc.scalar.activation(out=pair(i), in_=pair(i), func=ACT.Silu)
             nc.sync.dma_start(out=d_v[:, i : i + 2, :], in_=et[i // G][:, i % G : i % G + 2, :])
 
-        LEAD_SQ = 8
-        LEAD_C = 6
+        LEAD_C = 2
+        LEAD_A = 8
+        LEAD_S = 12
 
         def on(i):
             return 0 <= i < NT
 
         def step3(n):
             if on(n):
-                sq_dev(n)
-            if on(n - (LEAD_SQ - LEAD_C)):
-                centre(n - (LEAD_SQ - LEAD_C))
-            if on(n - LEAD_SQ):
-                affine(n - LEAD_SQ)
-            m = n - LEAD_SQ - 2
+                deviations(n)
+            if on(n - LEAD_C):
+                centre(n - LEAD_C)
+            if on(n - 1):
+                group_rstd(n - 1)
+            if on(n - LEAD_A):
+                affine(n - LEAD_A)
+            m = n - LEAD_S
             if on(m) and m % 2 == 0:
                 silu_store(m)
 
@@ -382,18 +435,14 @@ def tile_latentvaeblock_pa_t_kernel(
                 steps[0] += 1
 
         FILL = 8
-        DRAIN = 7
-        MU = 6
-        mm_mu(0)
+        DRAIN = 8
         for k in range(-FILL, NT + DRAIN):
+            if k >= 0 and on(mus[0]):
+                mm_mu(mus[0])
+            if on(k + 6):
+                mm_lv(k + 6)
             if on(k - 7):
                 mm2(k - 7)
-            if on(k + 6):
-                mm_lv(k + 6, ps_lv, "lv")
-            if on(k + MU + 1) and k + MU + 1 > 0:
-                mm_mu(k + MU + 1)
-            if on(k + 1):
-                warm_up(k + 1)
             if k % 2 == 0 and on(k - 4):
                 tr_z((k - 4) // 2)
             if on(k + 1):
@@ -402,29 +451,33 @@ def tile_latentvaeblock_pa_t_kernel(
                 kl_scale_sums(k)
             if k % 2 == 0 and on(k + 8):
                 ln1(k + 8)
-            if k % 2 == 1 and on(k - 5):
-                ev_z((k - 5) // 2)
             if on(k + 5):
                 guard(k + 5)
+            if on(k - 1):
+                scale_noise(k - 1)
+            if k % 2 == 1 and on(k - 5):
+                ev_z((k - 5) // 2)
+            if k % 2 == 0 and on(k - 6):
+                q_z((k - 6) // 2)
             if on(k - 1):
                 sample(k - 1)
                 if k % 2 == 0:
                     round_z((k - 2) // 2)
             if k % G == 1 and 2 <= k // G + 2 < NG:
                 load_n(k // G + 2)
-            if on(k + MU):
-                mu_add(k + MU)
-            if k % 2 == 0 and on(k - 6):
-                q_z((k - 6) // 2)
+            if k >= 0:
+                next_mu()
+            if on(k - 8):
+                mean(k - 8)
             if on(k - 7):
                 pre_add(k - 7)
-            if on(k):
-                scale_noise(k)
-            if on(k + MU - 1):
-                kl_mu_sum(k + MU - 1)
+            if on(k + 5):
+                kl_mu_sum(k + 5)
+            if k == NT - 5:
+                spread_gb()
             if k >= NT:
-                run_steps(3)
-            elif k >= 25:
+                run_steps(2)
+            elif k >= NT - 10:
                 run_steps(1)
 
         nc.gpsimd.tensor_tensor(out=kl_a[:], in0=sums2[:], in1=summu[:], op=ALU.add)
@@ -432,4 +485,4 @@ def tile_latentvaeblock_pa_t_kernel(
         nc.gpsimd.tensor_tensor(out=kl_c[:], in0=kl_b[:], in1=sumln[:], op=ALU.subtract)
         nc.sync.dma_start(out=kl_v, in_=kl_c[:])
 
-        run_steps(NT + LEAD_SQ + 2 - steps[0])
+        run_steps(NT + LEAD_S - steps[0])

@@ -44,7 +44,7 @@ def tile_latentvaeblock_pa_t_kernel(
         hst = ctx.enter_context(tc.tile_pool(name="hst", bufs=4))
         nst = ctx.enter_context(tc.tile_pool(name="nst", bufs=3))
         grp = ctx.enter_context(tc.tile_pool(name="grp", bufs=3))
-        mup = ctx.enter_context(tc.tile_pool(name="mup", bufs=20))
+        mup = ctx.enter_context(tc.tile_pool(name="mup", bufs=16))
         snp = ctx.enter_context(tc.tile_pool(name="snp", bufs=3))
         ps_lv = ctx.enter_context(tc.psum_pool(name="ps_lv", bufs=2))
         ps_sr = ctx.enter_context(tc.psum_pool(name="ps_sr", bufs=3))
@@ -198,7 +198,7 @@ def tile_latentvaeblock_pa_t_kernel(
         mus = [0]
 
         def mm_mu(i):
-            mup_ps[i] = ps_1.tile([P, D], F32, name="accmu", tag=("mu", "z", "mm2")[i % 3] if i < 8 else "mu")
+            mup_ps[i] = ps_1.tile([P, D], F32, name="accmu", tag=("mu", "z", "mm2")[i % 3] if i < 14 else ("mu", "mm2")[i % 2] if i < 18 else "mu")
             cols = slice(i * P, (i + 1) * P)
             mx(mup_ps[i][:], hc[:, cols], hs[:, cols], w1c[:, 0:D], w1s[:, 0:D])
 
@@ -333,7 +333,7 @@ def tile_latentvaeblock_pa_t_kernel(
         def ev_z(j):
             zg[j] = grp.tile([P, 2, P, 2], F32, name="zg", align_bytes=64)
             src = zps[j][:].rearrange("p (j u) r -> p j r u", u=2)
-            if j % 3 == 0:
+            if j % 2 == 0:
                 nc.scalar.copy(out=zg[j][:], in_=src)
             else:
                 nc.vector.tensor_copy(out=zg[j][:], in_=src)
@@ -362,7 +362,7 @@ def tile_latentvaeblock_pa_t_kernel(
         def mean(i):
             if i % NEG == NEG - 1:
                 cols = slice(i + 1 - NEG, i + 1)
-                nc.vector.tensor_scalar(out=negmean[:, cols], in0=sumpre[:, cols], scalar1=-1.0 / D, scalar2=None, op0=ALU.mult)
+                nc.scalar.mul(out=negmean[:, cols], in_=sumpre[:, cols], mul=-1.0 / D)
                 for t in range(i + 1 - NEG, i + 1):
                     have_mean.add(t)
 
@@ -393,7 +393,7 @@ def tile_latentvaeblock_pa_t_kernel(
             )
 
         def affine(i):
-            if i % 4 == 1:
+            if on_g(i):
                 nc.gpsimd.tensor_scalar(
                     out=xrow(i), in0=xrow(i), scalar1=rstd[:, i : i + 1], scalar2=0.0, op0=ALU.mult, op1=ALU.add
                 )
@@ -407,6 +407,7 @@ def tile_latentvaeblock_pa_t_kernel(
             nc.scalar.activation(out=pair(i), in_=pair(i), func=ACT.Silu)
             nc.sync.dma_start(out=d_v[:, i : i + 2, :], in_=et[i // G][:, i % G : i % G + 2, :])
 
+        LEAD_G = 6
         LEAD_C = 2
         LEAD_A = 8
         LEAD_S = 12
@@ -414,14 +415,19 @@ def tile_latentvaeblock_pa_t_kernel(
         def on(i):
             return 0 <= i < NT
 
+        def on_g(i):
+            return 6 <= i < NT - 4 and i % 8 in (1, 4, 6)
+
         def step3(n):
             if on(n):
                 deviations(n)
             if on(n - LEAD_C):
                 centre(n - LEAD_C)
-            if on(n - 1):
-                group_rstd(n - 1)
-            if on(n - LEAD_A):
+            if on(n - 2):
+                group_rstd(n - 2)
+            if on_g(n - LEAD_G):
+                affine(n - LEAD_G)
+            if on(n - LEAD_A) and not on_g(n - LEAD_A):
                 affine(n - LEAD_A)
             m = n - LEAD_S
             if on(m) and m % 2 == 0:
@@ -439,6 +445,8 @@ def tile_latentvaeblock_pa_t_kernel(
         for k in range(-FILL, NT + DRAIN):
             if k >= 0 and on(mus[0]):
                 mm_mu(mus[0])
+            if 0 <= k < 5:
+                mm_mu(mus[0] + 1)
             if on(k + 6):
                 mm_lv(k + 6)
             if on(k - 7):
@@ -451,6 +459,8 @@ def tile_latentvaeblock_pa_t_kernel(
                 kl_scale_sums(k)
             if k % 2 == 0 and on(k + 8):
                 ln1(k + 8)
+            if on(k - 8):
+                mean(k - 8)
             if on(k + 5):
                 guard(k + 5)
             if on(k - 1):
@@ -467,8 +477,8 @@ def tile_latentvaeblock_pa_t_kernel(
                 load_n(k // G + 2)
             if k >= 0:
                 next_mu()
-            if on(k - 8):
-                mean(k - 8)
+            if 0 <= k < 5:
+                next_mu()
             if on(k - 7):
                 pre_add(k - 7)
             if on(k + 5):
@@ -476,8 +486,8 @@ def tile_latentvaeblock_pa_t_kernel(
             if k == NT - 5:
                 spread_gb()
             if k >= NT:
-                run_steps(2)
-            elif k >= NT - 10:
+                run_steps(3)
+            elif k >= NT - 5:
                 run_steps(1)
 
         nc.gpsimd.tensor_tensor(out=kl_a[:], in0=sums2[:], in1=summu[:], op=ALU.add)

@@ -84,6 +84,7 @@ def tile_latentvaeblock_pa_t_kernel(
         w2s = const.tile([P, D], U8, name="w2s", align_bytes=64)
         hc = const.tile([P, NT * P], U32, name="hc", align_bytes=64)
         hs = const.tile([P, NT * P], U8, name="hs", align_bytes=64)
+        junk_v = const.tile([P, D], BF16, name="junk_v")
         junk = [const.tile([P, D], BF16, name="junk%d" % q) for q in range(4)]
         sumln = const.tile([P, NT], F32, name="sumln")
         sums2 = const.tile([P, NT], F32, name="sums2")
@@ -308,6 +309,11 @@ def tile_latentvaeblock_pa_t_kernel(
             nc.scalar.activation(out=junk[0][:], in_=srow[i][:], func=ACT.Ln, scale=-1.0, accum_out=sumln[:, i : i + 1])
             nc.scalar.activation(out=junk[1][:], in_=srow[i][:], func=ACT.Square, accum_out=sums2[:, i : i + 1])
 
+        def kl_mu_sum_v(i):
+            nc.vector.scalar_tensor_tensor(
+                out=junk_v[:], in0=mu[i][:], scalar=1.0, in1=mu[i][:], op0=ALU.mult, op1=ALU.mult, accum_out=summu[:, i : i + 1]
+            )
+
         def kl_mu_sum(i):
             nc.scalar.activation(out=junk[2][:], in_=mu[i][:], func=ACT.Square, accum_out=summu[:, i : i + 1])
 
@@ -333,7 +339,7 @@ def tile_latentvaeblock_pa_t_kernel(
         def ev_z(j):
             zg[j] = grp.tile([P, 2, P, 2], F32, name="zg", align_bytes=64)
             src = zps[j][:].rearrange("p (j u) r -> p j r u", u=2)
-            if j % 2 == 0:
+            if j % 2 == 1:
                 nc.scalar.copy(out=zg[j][:], in_=src)
             else:
                 nc.vector.tensor_copy(out=zg[j][:], in_=src)
@@ -404,6 +410,11 @@ def tile_latentvaeblock_pa_t_kernel(
                 )
 
         def silu_store(i):
+            if i == NT - 2:
+                for t in (i, i + 1):
+                    nc.scalar.activation(out=xrow(t), in_=xrow(t), func=ACT.Silu)
+                    nc.sync.dma_start(out=d_v[:, t, :], in_=xrow(t))
+                return
             nc.scalar.activation(out=pair(i), in_=pair(i), func=ACT.Silu)
             nc.sync.dma_start(out=d_v[:, i : i + 2, :], in_=et[i // G][:, i % G : i % G + 2, :])
 
@@ -416,7 +427,7 @@ def tile_latentvaeblock_pa_t_kernel(
             return 0 <= i < NT
 
         def on_g(i):
-            return 6 <= i < NT - 4 and i % 8 in (1, 4, 6)
+            return 8 <= i < NT - 4 and i % 8 in (1, 4, 6)
 
         def step3(n):
             if on(n):
@@ -441,6 +452,7 @@ def tile_latentvaeblock_pa_t_kernel(
                 steps[0] += 1
 
         FILL = 8
+        MU_V = 5
         DRAIN = 8
         for k in range(-FILL, NT + DRAIN):
             if k >= 0 and on(mus[0]):
@@ -457,12 +469,17 @@ def tile_latentvaeblock_pa_t_kernel(
                 tr_s(k + 1)
             if on(k):
                 kl_scale_sums(k)
-            if k % 2 == 0 and on(k + 8):
-                ln1(k + 8)
+            if k == -FILL:
+                for q in range(0, 8, 2):
+                    ln1(q)
+            elif k % 2 == 0 and on(k + 14):
+                ln1(k + 14)
             if on(k - 8):
                 mean(k - 8)
             if on(k + 5):
                 guard(k + 5)
+            if 0 <= k + 5 < MU_V:
+                kl_mu_sum_v(k + 5)
             if on(k - 1):
                 scale_noise(k - 1)
             if k % 2 == 1 and on(k - 5):
@@ -481,13 +498,13 @@ def tile_latentvaeblock_pa_t_kernel(
                 next_mu()
             if on(k - 7):
                 pre_add(k - 7)
-            if on(k + 5):
+            if MU_V <= k + 5 < NT:
                 kl_mu_sum(k + 5)
             if k == NT - 5:
                 spread_gb()
             if k >= NT:
                 run_steps(3)
-            elif k >= NT - 5:
+            elif k >= NT - 6:
                 run_steps(1)
 
         nc.gpsimd.tensor_tensor(out=kl_a[:], in0=sums2[:], in1=summu[:], op=ALU.add)

@@ -41,10 +41,9 @@ def tile_latentvaeblock_pa_t_kernel(
         const = ctx.enter_context(tc.tile_pool(name="const", bufs=1))
         big = ctx.enter_context(tc.tile_pool(name="big", bufs=1))
         wst = ctx.enter_context(tc.tile_pool(name="wst", bufs=4))
-        hst = ctx.enter_context(tc.tile_pool(name="hst", bufs=4))
-        nst = ctx.enter_context(tc.tile_pool(name="nst", bufs=3))
+        hst = ctx.enter_context(tc.tile_pool(name="hst", bufs=5))
         grp = ctx.enter_context(tc.tile_pool(name="grp", bufs=3))
-        mup = ctx.enter_context(tc.tile_pool(name="mup", bufs=16))
+        mup = ctx.enter_context(tc.tile_pool(name="mup", bufs=20))
         snp = ctx.enter_context(tc.tile_pool(name="snp", bufs=3))
         ps_lv = ctx.enter_context(tc.psum_pool(name="ps_lv", bufs=2))
         ps_sr = ctx.enter_context(tc.psum_pool(name="ps_sr", bufs=3))
@@ -73,9 +72,11 @@ def tile_latentvaeblock_pa_t_kernel(
         b_all = const.tile([P, D], BF16, name="b_all")
         g_all = const.tile([P, D], BF16, name="g_all")
         ones = const.tile([P, P], BF16, name="ones")
+        zeros = const.tile([P, D], BF16, name="zeros")
+        nc.gpsimd.memset(ones[:], 1.0)
+        nc.gpsimd.memset(zeros[:], 0.0)
         nc.gpsimd.memset(g_row[:], 0.0)
         nc.gpsimd.memset(b_row[:], 0.0)
-        nc.gpsimd.memset(ones[:], 1.0)
         bcol = const.tile([P, G], F32, name="bcol")
         bcol2 = const.tile([P, G], F32, name="bcol2")
         w1c = const.tile([P, 2 * D], U32, name="w1c", align_bytes=64)
@@ -107,7 +108,7 @@ def tile_latentvaeblock_pa_t_kernel(
         nch = {}
 
         def load_h(c, parts=1):
-            hch[c] = hst.tile([P, G, D], BF16, name="hch")
+            hch[c] = hst.tile([P, G, D], BF16, name="hch", tag="rows")
             step = G // parts
             for q in range(parts):
                 nc.sync.dma_start(
@@ -115,7 +116,7 @@ def tile_latentvaeblock_pa_t_kernel(
                 )
 
         def load_n(c):
-            nch[c] = nst.tile([P, G, D], BF16, name="nch")
+            nch[c] = hst.tile([P, G, D], BF16, name="nch", tag="rows")
             nc.sync.dma_start(out=nch[c][:], in_=n_v[:, c * G : (c + 1) * G, :])
 
         wraw = {}
@@ -191,15 +192,24 @@ def tile_latentvaeblock_pa_t_kernel(
             else:
                 nc.vector.tensor_copy(out=dst, in_=src)
 
+        def quant_lv(half):
+            cols = slice(D + half * D // 2, D + (half + 1) * D // 2)
+            nc.vector.quantize_mx(
+                out=w1c[:, cols].bitcast(FP8X4),
+                scales=w1s[:, cols],
+                in_=wgs["lv"][:, half * D // 2 : (half + 1) * D // 2, :].rearrange("p c t -> p (c t)"),
+            )
+
         def quant_w(wg, codes, scales):
             nc.vector.quantize_mx(out=codes.bitcast(FP8X4), scales=scales, in_=wg[:].rearrange("p c t -> p (c t)"))
 
         mup_ps = {}
+        mu_tags = ["mu", "z", "mm2"]
         mu = {}
         mus = [0]
 
         def mm_mu(i):
-            mup_ps[i] = ps_1.tile([P, D], F32, name="accmu", tag=("mu", "z", "mm2")[i % 3] if i < 14 else ("mu", "mm2")[i % 2] if i < 18 else "mu")
+            mup_ps[i] = ps_1.tile([P, D], F32, name="accmu", tag=mu_tags[i % len(mu_tags)])
             cols = slice(i * P, (i + 1) * P)
             mx(mup_ps[i][:], hc[:, cols], hs[:, cols], w1c[:, 0:D], w1s[:, 0:D])
 
@@ -212,8 +222,8 @@ def tile_latentvaeblock_pa_t_kernel(
                 mu_add(mus[0])
                 mus[0] += 1
 
-        load_w("lv", enc_w_out[:, D : 2 * D])
         load_h(0, parts=2)
+        load_w("lv", enc_w_out[:, D : 2 * D])
         load_h(1)
         load_h(2)
         load_h(3)
@@ -225,21 +235,31 @@ def tile_latentvaeblock_pa_t_kernel(
         nc.sync.dma_start(out=g_all[:], in_=dec_ln_g.partition_broadcast(P))
         nc.sync.dma_start(out=g_row[0:1, :], in_=dec_ln_g.rearrange("(o n) -> o n", o=1))
         nc.sync.dma_start(out=b_row[0:1, :], in_=dec_ln_b.rearrange("(o n) -> o n", o=1))
+        warm_ps = ps_lv.tile([P, D], F32, name="warm_ps", tag="lv")
+
+        def keep_busy(count):
+            for q in range(count):
+                nc.tensor.matmul(out=warm_ps[:], lhsT=ones[:], rhs=zeros[:], start=True, stop=True)
+
+        keep_busy(6)
         tr_h(0)
         tr_h(1)
+        keep_busy(2)
         bps = ps_sr.tile([P, P], BF16, name="bps", tag="sr")
         nc.tensor.transpose(bps[:], vecs[:], identb[:])
         tr_h(2)
+        keep_busy(2)
         tr_h(3)
         regroup_w("lv", 0)
         regroup_w("lv", 1)
         ev_h(0)
         ev_h(1)
-        quant_w(wgs["lv"], w1c[:, D : 2 * D], w1s[:, D : 2 * D])
         q_h(0)
+        quant_lv(0)
         nc.vector.tensor_scalar(out=bcol[:], in0=bps[:, 0:G], scalar1=-1.0, scalar2=None, op0=ALU.mult)
         nc.vector.tensor_scalar(out=bcol2[:], in0=bps[:, 0:G], scalar1=-1.0, scalar2=-SCALE_EPS, op0=ALU.mult, op1=ALU.add)
         q_h(1)
+        quant_lv(1)
         for u in range(G):
             mm_lv(u, wide=True)
         ev_h(2)
@@ -267,12 +287,13 @@ def tile_latentvaeblock_pa_t_kernel(
             if g == 4:
                 quant_w(wgs["dec"], w2c[:], w2s[:])
             for n in range(G):
+                if g >= NG - 2:
+                    for q in range(1 + n % 2):
+                        mm_mu(mus[0])
+                        next_mu()
                 exp_lv(G * g + n)
                 if g + 1 < NG:
                     mm_lv(G * (g + 1) + n, wide=True)
-                if g >= NG - 2:
-                    mm_mu(mus[0])
-                    next_mu()
             if g == 5:
                 load_n(0)
             if g == 6:
@@ -284,8 +305,6 @@ def tile_latentvaeblock_pa_t_kernel(
         zb = {}
         zps = {}
         zg = {}
-        zc = {}
-        zs = {}
         pps = {}
 
         def ln1(u):
@@ -345,17 +364,16 @@ def tile_latentvaeblock_pa_t_kernel(
                 nc.vector.tensor_copy(out=zg[j][:], in_=src)
 
         def q_z(j):
-            zc[j] = grp.tile([P, 2 * P], U32, name="zc", align_bytes=64)
-            zs[j] = grp.tile([P, 2 * P], U8, name="zs", align_bytes=64)
+            cols = slice(2 * j * P, (2 * j + 2) * P)
             nc.vector.quantize_mx(
-                out=zc[j][:].bitcast(FP8X4), scales=zs[j][:], in_=zg[j][:].rearrange("p j r u -> p (j r u)").bitcast(BF16)
+                out=hc[:, cols].bitcast(FP8X4), scales=hs[:, cols], in_=zg[j][:].rearrange("p j r u -> p (j r u)").bitcast(BF16)
             )
 
         def mm2(i):
             late = i >= 17 and i % 2 == 1
             pps[i] = ps_1.tile([P, D], F32, name="acc2", tag="mu" if late else "mm2")
-            cols = slice((i % 2) * P, (i % 2 + 1) * P)
-            mx(pps[i][:], zc[i // 2][:, cols], zs[i // 2][:, cols], w2c[:], w2s[:])
+            cols = slice(i * P, (i + 1) * P)
+            mx(pps[i][:], hc[:, cols], hs[:, cols], w2c[:], w2s[:])
 
         NEG = 4
         have_mean = set()
@@ -455,6 +473,10 @@ def tile_latentvaeblock_pa_t_kernel(
         MU_V = 5
         DRAIN = 8
         for k in range(-FILL, NT + DRAIN):
+            if k == 4:
+                mu_tags.remove("z")
+            if k == 6:
+                mu_tags.remove("mm2")
             if k >= 0 and on(mus[0]):
                 mm_mu(mus[0])
             if 0 <= k < 5:

@@ -45,6 +45,7 @@ def tile_latentvaeblock_pa_t_kernel(
         grp = ctx.enter_context(tc.tile_pool(name="grp", bufs=3))
         mup = ctx.enter_context(tc.tile_pool(name="mup", bufs=20))
         snp = ctx.enter_context(tc.tile_pool(name="snp", bufs=3))
+        dgp = ctx.enter_context(tc.tile_pool(name="dgp", bufs=3))
         ps_lv = ctx.enter_context(tc.psum_pool(name="ps_lv", bufs=2))
         ps_sr = ctx.enter_context(tc.psum_pool(name="ps_sr", bufs=3))
         ps_1 = ctx.enter_context(tc.psum_pool(name="ps_1", bufs=1))
@@ -69,8 +70,6 @@ def tile_latentvaeblock_pa_t_kernel(
         b_dec = const.tile([P, D], BF16, name="b_dec")
         g_row = const.tile([P, D], BF16, name="g_row")
         b_row = const.tile([P, D], BF16, name="b_row")
-        b_all = const.tile([P, D], BF16, name="b_all")
-        g_all = const.tile([P, D], BF16, name="g_all")
         ones = const.tile([P, P], BF16, name="ones")
         zeros = const.tile([P, D], BF16, name="zeros")
         nc.gpsimd.memset(ones[:], 1.0)
@@ -231,8 +230,6 @@ def tile_latentvaeblock_pa_t_kernel(
         load_w("dec", dec_w_in)
         nc.sync.dma_start(out=b_mu[:], in_=enc_b_out[0:D].partition_broadcast(P))
         nc.sync.dma_start(out=b_dec[:], in_=dec_b_in.partition_broadcast(P))
-        nc.sync.dma_start(out=b_all[:], in_=dec_ln_b.partition_broadcast(P))
-        nc.sync.dma_start(out=g_all[:], in_=dec_ln_g.partition_broadcast(P))
         nc.sync.dma_start(out=g_row[0:1, :], in_=dec_ln_g.rearrange("(o n) -> o n", o=1))
         nc.sync.dma_start(out=b_row[0:1, :], in_=dec_ln_b.rearrange("(o n) -> o n", o=1))
         warm_ps = ps_lv.tile([P, D], F32, name="warm_ps", tag="lv")
@@ -413,19 +410,27 @@ def tile_latentvaeblock_pa_t_kernel(
 
         def centre(i):
             nc.vector.scalar_tensor_tensor(
-                out=xrow(i), in0=xrow(i), scalar=negmean[:, i : i + 1], in1=gb_ps.get("g", g_all)[:], op0=ALU.add, op1=ALU.mult
+                out=xrow(i), in0=xrow(i), scalar=negmean[:, i : i + 1], in1=gb_ps["g"][:], op0=ALU.add, op1=ALU.mult
             )
 
+        diag = {}
+        yps = {}
+
+        def make_diag(i):
+            diag[i] = dgp.tile([P, P], F32, name="diag")
+            nc.gpsimd.tensor_scalar(
+                out=diag[i][:], in0=ident[:], scalar1=rstd[:, i : i + 1], scalar2=0.0, op0=ALU.mult, op1=ALU.add
+            )
+
+        def affine_t(i):
+            yps[i] = ps_sr.tile([P, D], F32, name="yps", tag="sr")
+            nc.tensor.matmul(out=yps[i][:], lhsT=ones[:], rhs=b_row[:], start=True, stop=False)
+            nc.tensor.matmul(out=yps[i][:], lhsT=diag[i][:], rhs=xrow(i), start=False, stop=True)
+
         def affine(i):
-            if on_g(i):
-                nc.gpsimd.tensor_scalar(
-                    out=xrow(i), in0=xrow(i), scalar1=rstd[:, i : i + 1], scalar2=0.0, op0=ALU.mult, op1=ALU.add
-                )
-                nc.gpsimd.tensor_tensor(out=xrow(i), in0=xrow(i), in1=b_all[:], op=ALU.add)
-            else:
-                nc.vector.scalar_tensor_tensor(
-                    out=xrow(i), in0=xrow(i), scalar=rstd[:, i : i + 1], in1=gb_ps["b"][:], op0=ALU.mult, op1=ALU.add
-                )
+            nc.vector.scalar_tensor_tensor(
+                out=xrow(i), in0=xrow(i), scalar=rstd[:, i : i + 1], in1=gb_ps["b"][:], op0=ALU.mult, op1=ALU.add
+            )
 
         def silu_store(i):
             if i == NT - 2:
@@ -433,10 +438,13 @@ def tile_latentvaeblock_pa_t_kernel(
                     nc.scalar.activation(out=xrow(t), in_=xrow(t), func=ACT.Silu)
                     nc.sync.dma_start(out=d_v[:, t, :], in_=xrow(t))
                 return
-            nc.scalar.activation(out=pair(i), in_=pair(i), func=ACT.Silu)
+            if on_t(i) or on_t(i + 1):
+                for t in (i, i + 1):
+                    nc.scalar.activation(out=xrow(t), in_=yps[t][:] if on_t(t) else xrow(t), func=ACT.Silu)
+            else:
+                nc.scalar.activation(out=pair(i), in_=pair(i), func=ACT.Silu)
             nc.sync.dma_start(out=d_v[:, i : i + 2, :], in_=et[i // G][:, i % G : i % G + 2, :])
 
-        LEAD_G = 6
         LEAD_C = 2
         LEAD_A = 8
         LEAD_S = 12
@@ -444,8 +452,11 @@ def tile_latentvaeblock_pa_t_kernel(
         def on(i):
             return 0 <= i < NT
 
-        def on_g(i):
-            return 8 <= i < NT - 4 and i % 8 in (1, 4, 6)
+        LEAD_D = 6
+        LEAD_T = 10
+
+        def on_t(i):
+            return 8 <= i < NT - 2 and i % 2 == 0
 
         def step3(n):
             if on(n):
@@ -454,9 +465,11 @@ def tile_latentvaeblock_pa_t_kernel(
                 centre(n - LEAD_C)
             if on(n - 2):
                 group_rstd(n - 2)
-            if on_g(n - LEAD_G):
-                affine(n - LEAD_G)
-            if on(n - LEAD_A) and not on_g(n - LEAD_A):
+            if on_t(n - LEAD_D):
+                make_diag(n - LEAD_D)
+            if on_t(n - LEAD_T):
+                affine_t(n - LEAD_T)
+            if on(n - LEAD_A) and not on_t(n - LEAD_A):
                 affine(n - LEAD_A)
             m = n - LEAD_S
             if on(m) and m % 2 == 0:

@@ -446,7 +446,7 @@ def tile_latentvaeblock_pa_t_kernel(
             nc.sync.dma_start(out=d_v[:, i : i + 2, :], in_=et[i // G][:, i % G : i % G + 2, :])
 
         LEAD_C = 2
-        LEAD_A = 8
+        LEAD_A = 7
         LEAD_S = 12
 
         def on(i):
@@ -456,7 +456,7 @@ def tile_latentvaeblock_pa_t_kernel(
         LEAD_T = 10
 
         def on_t(i):
-            return 8 <= i < NT - 2 and i % 2 == 0
+            return 4 <= i < NT - 2 and i % 2 == 0
 
         def step3(n):
             if on(n):
@@ -483,7 +483,7 @@ def tile_latentvaeblock_pa_t_kernel(
                 steps[0] += 1
 
         FILL = 8
-        MU_V = 5
+        MU_V = 6
         DRAIN = 8
         for k in range(-FILL, NT + DRAIN):
             if k == 4:

@@ -228,10 +228,6 @@ def tile_latentvaeblock_pa_t_kernel(
         load_h(3)
         load_w("mu", enc_w_out[:, 0:D])
         load_w("dec", dec_w_in)
-        nc.sync.dma_start(out=b_mu[:], in_=enc_b_out[0:D].partition_broadcast(P))
-        nc.sync.dma_start(out=b_dec[:], in_=dec_b_in.partition_broadcast(P))
-        nc.sync.dma_start(out=g_row[0:1, :], in_=dec_ln_g.rearrange("(o n) -> o n", o=1))
-        nc.sync.dma_start(out=b_row[0:1, :], in_=dec_ln_b.rearrange("(o n) -> o n", o=1))
         warm_ps = ps_lv.tile([P, D], F32, name="warm_ps", tag="lv")
 
         def keep_busy(count):
@@ -270,6 +266,11 @@ def tile_latentvaeblock_pa_t_kernel(
                 tr_h(2 * g + 5)
                 if g + 5 < NG:
                     load_h(g + 5)
+                if g + 5 == NG:
+                    nc.sync.dma_start(out=b_mu[:], in_=enc_b_out[0:D].partition_broadcast(P))
+                    nc.sync.dma_start(out=b_dec[:], in_=dec_b_in.partition_broadcast(P))
+                    nc.sync.dma_start(out=g_row[0:1, :], in_=dec_ln_g.rearrange("(o n) -> o n", o=1))
+                    nc.sync.dma_start(out=b_row[0:1, :], in_=dec_ln_b.rearrange("(o n) -> o n", o=1))
             if g + 2 < NG:
                 ev_h(2 * g + 4)
                 ev_h(2 * g + 5)
@@ -383,7 +384,9 @@ def tile_latentvaeblock_pa_t_kernel(
         def mean(i):
             if i % NEG == NEG - 1:
                 cols = slice(i + 1 - NEG, i + 1)
-                nc.scalar.mul(out=negmean[:, cols], in_=sumpre[:, cols], mul=-1.0 / D)
+                nc.gpsimd.tensor_scalar(
+                    out=negmean[:, cols], in0=sumpre[:, cols], scalar1=-1.0 / D, scalar2=0.0, op0=ALU.mult, op1=ALU.add
+                )
                 for t in range(i + 1 - NEG, i + 1):
                     have_mean.add(t)
 

@@ -226,8 +226,7 @@ def tile_latentvaeblock_pa_t_kernel(
         load_h(1)
         load_h(2)
         load_h(3)
-        load_w("mu", enc_w_out[:, 0:D])
-        load_w("dec", dec_w_in)
+        load_h(4)
         warm_ps = ps_lv.tile([P, D], F32, name="warm_ps", tag="lv")
 
         def keep_busy(count):
@@ -259,13 +258,16 @@ def tile_latentvaeblock_pa_t_kernel(
         ev_h(3)
         q_h(2)
         q_h(3)
-        load_h(4)
         for g in range(NG):
             if g + 2 < NG:
                 tr_h(2 * g + 4)
                 tr_h(2 * g + 5)
                 if g + 5 < NG:
                     load_h(g + 5)
+                if g == 0:
+                    load_w("mu", enc_w_out[:, 0:D])
+                if g == 2:
+                    load_w("dec", dec_w_in)
                 if g + 5 == NG:
                     nc.sync.dma_start(out=b_mu[:], in_=enc_b_out[0:D].partition_broadcast(P))
                     nc.sync.dma_start(out=b_dec[:], in_=dec_b_in.partition_broadcast(P))
@@ -276,13 +278,13 @@ def tile_latentvaeblock_pa_t_kernel(
                 ev_h(2 * g + 5)
                 q_h(2 * g + 4)
                 q_h(2 * g + 5)
-            if g < 2:
-                regroup_w("mu", g)
-            elif g < 4:
-                regroup_w("dec", g - 2)
-            if g == 2:
+            if 1 <= g < 3:
+                regroup_w("mu", g - 1)
+            elif 3 <= g < 5:
+                regroup_w("dec", g - 3)
+            if g == 3:
                 quant_w(wgs["mu"], w1c[:, 0:D], w1s[:, 0:D])
-            if g == 4:
+            if g == 5:
                 quant_w(wgs["dec"], w2c[:], w2s[:])
             for n in range(G):
                 if g >= NG - 2:

import math
from contextlib import ExitStack

import concourse.mybir as mybir
from concourse.masks import make_identity

F32 = mybir.dt.float32
BF16 = mybir.dt.bfloat16
U32 = mybir.dt.uint32
U8 = mybir.dt.uint8
FP8X4 = mybir.dt.float8_e4m3fn_x4
ALU = mybir.AluOpType
ACT = mybir.ActivationFunctionType

P = 128
ROWS = 4096
D = 512
NT = ROWS // P
G = 4
NG = NT // G
NP = NT // 2
LN_EPS = 1e-5
SCALE_EPS = 1e-5
SIG_FLOOR = 2.0**-62

FLOPS = 2 * ROWS * D * (2 * D) + 2 * ROWS * D * D


def tile_latentvaeblock_pa_t_kernel(
    tc, h_enc, noise, enc_w_out, enc_b_out, dec_w_in, dec_b_in, dec_ln_g, dec_ln_b, out_0, out_1, out_2
):
    nc = tc.nc
    h_v = h_enc.rearrange("(p t) k -> p t k", t=NT)
    n_v = noise.rearrange("(p t) k -> p t k", t=NT)
    z_v = out_0.rearrange("(p t) k -> p t k", t=NT)
    d_v = out_1.rearrange("(p t) k -> p t k", t=NT)
    kl_v = out_2.rearrange("(p t) -> p t", t=NT)

    with ExitStack() as ctx:
        ctx.enter_context(tc.manual_schedule())
        const = ctx.enter_context(tc.tile_pool(name="const", bufs=1))
        big = ctx.enter_context(tc.tile_pool(name="big", bufs=1))
        wst = ctx.enter_context(tc.tile_pool(name="wst", bufs=4))
        hst = ctx.enter_context(tc.tile_pool(name="hst", bufs=5))
        grp = ctx.enter_context(tc.tile_pool(name="grp", bufs=3))
        mup = ctx.enter_context(tc.tile_pool(name="mup", bufs=20))
        snp = ctx.enter_context(tc.tile_pool(name="snp", bufs=3))
        dgp = ctx.enter_context(tc.tile_pool(name="dgp", bufs=3))
        ps_lv = ctx.enter_context(tc.psum_pool(name="ps_lv", bufs=2))
        ps_sr = ctx.enter_context(tc.psum_pool(name="ps_sr", bufs=3))
        ps_1 = ctx.enter_context(tc.psum_pool(name="ps_1", bufs=1))

        ident = const.tile([P, P], F32, name="ident")
        make_identity(nc, ident[:])
        identb = const.tile([P, P], BF16, name="identb")
        vecs = const.tile([P, P], BF16, name="vecs")
        one_t = const.tile([P, 1], F32, name="one_t")
        warm = const.tile([P, 1], F32, name="warm")
        floor_t = const.tile([P, 1], F32, name="floor_t")
        mhalf = const.tile([P, G], F32, name="mhalf")
        nc.vector.memset(one_t[:], 1.0)
        nc.vector.memset(floor_t[:], SIG_FLOOR)
        nc.vector.memset(vecs[:], 0.0)
        nc.vector.memset(mhalf[:], -0.5)
        nc.scalar.dma_start(out=vecs[0:G, :], in_=enc_b_out[D : 2 * D].rearrange("(n p) -> n p", p=P))
        nc.scalar.activation(out=warm[:], in_=one_t[:], func=ACT.Sigmoid)
        nc.vector.tensor_copy(out=identb[:], in_=ident[:])

        b_mu = const.tile([P, D], BF16, name="b_mu")
        b_dec = const.tile([P, D], BF16, name="b_dec")
        g_row = const.tile([P, D], BF16, name="g_row")
        b_row = const.tile([P, D], BF16, name="b_row")
        ones = const.tile([P, P], BF16, name="ones")
        zeros = const.tile([P, D], BF16, name="zeros")
        nc.gpsimd.memset(ones[:], 1.0)
        nc.gpsimd.memset(zeros[:], 0.0)
        nc.gpsimd.memset(g_row[:], 0.0)
        nc.gpsimd.memset(b_row[:], 0.0)
        bcol = const.tile([P, G], F32, name="bcol")
        bcol2 = const.tile([P, G], F32, name="bcol2")
        w1c = const.tile([P, 2 * D], U32, name="w1c", align_bytes=64)
        w1s = const.tile([P, 2 * D], U8, name="w1s", align_bytes=64)
        w2c = const.tile([P, D], U32, name="w2c", align_bytes=64)
        w2s = const.tile([P, D], U8, name="w2s", align_bytes=64)
        hc = const.tile([P, NT * P], U32, name="hc", align_bytes=64)
        hs = const.tile([P, NT * P], U8, name="hs", align_bytes=64)
        junk_v = const.tile([P, D], BF16, name="junk_v")
        junk = [const.tile([P, D], BF16, name="junk%d" % q) for q in range(4)]
        sumln = const.tile([P, NT], F32, name="sumln")
        sums2 = const.tile([P, NT], F32, name="sums2")
        summu = const.tile([P, NT], F32, name="summu")
        sumdev = const.tile([P, NT], F32, name="sumdev")
        sumpre = const.tile([P, NT], F32, name="sumpre")
        negmean = const.tile([P, NT], F32, name="negmean")
        varep = const.tile([P, NT], F32, name="varep")
        rstd = const.tile([P, NT], F32, name="rstd")
        kl_a = const.tile([P, NT], F32, name="kl_a")
        kl_b = const.tile([P, NT], F32, name="kl_b")
        kl_c = const.tile([P, NT], F32, name="kl_c")

        et = [big.tile([P, G, D], F32, name="et%d" % g) for g in range(NG)]

        def xrow(i):
            return et[i // G][:, i % G, :]

        hch = {}
        nch = {}

        def load_h(c, parts=1):
            hch[c] = hst.tile([P, G, D], BF16, name="hch", tag="rows")
            step = G // parts
            for q in range(parts):
                nc.sync.dma_start(
                    out=hch[c][:, q * step : (q + 1) * step, :], in_=h_v[:, c * G + q * step : c * G + (q + 1) * step, :]
                )

        def load_n(c):
            nch[c] = hst.tile([P, G, D], BF16, name="nch", tag="rows")
            nc.sync.dma_start(out=nch[c][:], in_=n_v[:, c * G : (c + 1) * G, :])

        wraw = {}

        def load_w(which, w):
            wraw[which] = wst.tile([P, 4, D], BF16, name="wraw", tag="w", align_bytes=64)
            src = w.rearrange("(u p e) c -> u p e c", u=2, e=2)
            for u in range(2):
                nc.sync.dma_start(out=wraw[which][:, 2 * u : 2 * u + 2, :], in_=src[u])

        hps = {}
        hg = {}
        lvp = {}

        def tr_words(dst, rows):
            for u in range(2):
                nc.tensor.transpose(dst[:, u, :], rows.bitcast(F32)[:, u * P : (u + 1) * P], ident[:])

        def tr_h(j):
            if j == 3:
                hps[j] = ps_sr.tile([P, 4, P], F32, name="hps", tag="sr")
            else:
                hps[j] = ps_1.tile([P, 4, P], F32, name="hps", tag=("mu", "z", "mm2")[j % 3])
            for jj in range(2):
                i = 2 * j + jj
                tr_words(hps[j][:, 2 * jj : 2 * jj + 2, :], hch[i // G][:, i % G, :])

        def ev_h(j):
            hg[j] = grp.tile([P, 2, P, 2], F32, name="hg", align_bytes=64)
            src = hps[j][:].rearrange("p (j u) r -> p j r u", u=2)
            if j < 2:
                nc.scalar.copy(out=hg[j][:], in_=src)
            else:
                nc.vector.tensor_copy(out=hg[j][:], in_=src)

        def q_h(j):
            cols = slice(2 * j * P, (2 * j + 2) * P)
            nc.vector.quantize_mx(
                out=hc[:, cols].bitcast(FP8X4), scales=hs[:, cols], in_=hg[j][:].rearrange("p j r u -> p (j r u)").bitcast(BF16)
            )

        def mx(out, lc, ls, rc, rs):
            nc.tensor.matmul_mx(
                out=out, lhsT=lc.bitcast(FP8X4), lhsT_scale=ls, rhs=rc.bitcast(FP8X4), rhs_scale=rs, start=True, stop=True
            )

        def mm_lv(u, wide=False):
            if wide and u % G >= 2:
                lvp[u] = ps_sr.tile([P, D], F32, name="acc", tag="sr")
            else:
                lvp[u] = ps_lv.tile([P, D], F32, name="acc", tag="lv")
            wcols = slice(D + (u % G) * P, D + (u % G + 1) * P)
            rows = slice((u // G) * G * P, (u // G + 1) * G * P)
            mx(lvp[u][:], w1c[:, wcols], w1s[:, wcols], hc[:, rows], hs[:, rows])

        def exp_lv(u):
            n = u % G
            nc.scalar.activation(out=et[u // G][:, n, :], in_=lvp[u][:], func=ACT.Sigmoid, bias=bcol[:, n : n + 1])

        def pair(u):
            return et[u // G][:, u % G : u % G + 2, :].rearrange("p a c -> p (a c)")

        wgs = {}

        def regroup_w(which, half):
            if half == 0:
                wgs[which] = wst.tile([P, D, 4], BF16, name="wg", tag="w", align_bytes=64)
            cols = slice(half * D // 2, (half + 1) * D // 2)
            dst = wgs[which][:, cols, :].rearrange("p (c i) t -> p c t i", i=4)
            src = wraw[which][:, :, cols].rearrange("p t (c i) -> p c t i", i=4)
            if which == "lv":
                nc.vector.tensor_scalar(out=dst, in0=src, scalar1=-1.0, scalar2=None, op0=ALU.mult)
            else:
                nc.vector.tensor_copy(out=dst, in_=src)

        def quant_lv(half):
            cols = slice(D + half * D // 2, D + (half + 1) * D // 2)
            nc.vector.quantize_mx(
                out=w1c[:, cols].bitcast(FP8X4),
                scales=w1s[:, cols],
                in_=wgs["lv"][:, half * D // 2 : (half + 1) * D // 2, :].rearrange("p c t -> p (c t)"),
            )

        def quant_w(wg, codes, scales):
            nc.vector.quantize_mx(out=codes.bitcast(FP8X4), scales=scales, in_=wg[:].rearrange("p c t -> p (c t)"))

        mup_ps = {}
        mu_tags = ["mu", "z", "mm2"]
        mu = {}
        mus = [0]

        def mm_mu(i):
            mup_ps[i] = ps_1.tile([P, D], F32, name="accmu", tag=mu_tags[i % len(mu_tags)])
            cols = slice(i * P, (i + 1) * P)
            mx(mup_ps[i][:], hc[:, cols], hs[:, cols], w1c[:, 0:D], w1s[:, 0:D])

        def mu_add(i):
            mu[i] = mup.tile([P, D], F32, name="mu")
            nc.vector.tensor_tensor(out=mu[i][:], in0=b_mu[:], in1=mup_ps[i][:], op=ALU.add)

        def next_mu():
            if mus[0] < NT:
                mu_add(mus[0])
                mus[0] += 1

        load_h(0, parts=2)
        load_w("lv", enc_w_out[:, D : 2 * D])
        load_h(1)
        load_h(2)
        load_h(3)
        load_h(4)
        warm_ps = ps_lv.tile([P, D], F32, name="warm_ps", tag="lv")

        def keep_busy(count):
            for q in range(count):
                nc.tensor.matmul(out=warm_ps[:], lhsT=ones[:], rhs=zeros[:], start=True, stop=True)

        keep_busy(6)
        tr_h(0)
        tr_h(1)
        keep_busy(2)
        bps = ps_sr.tile([P, P], BF16, name="bps", tag="sr")
        nc.tensor.transpose(bps[:], vecs[:], identb[:])
        tr_h(2)
        keep_busy(2)
        tr_h(3)
        regroup_w("lv", 0)
        regroup_w("lv", 1)
        ev_h(0)
        ev_h(1)
        q_h(0)
        quant_lv(0)
        nc.vector.tensor_scalar(out=bcol[:], in0=bps[:, 0:G], scalar1=-1.0, scalar2=None, op0=ALU.mult)
        nc.vector.tensor_scalar(out=bcol2[:], in0=bps[:, 0:G], scalar1=-1.0, scalar2=-SCALE_EPS, op0=ALU.mult, op1=ALU.add)
        q_h(1)
        quant_lv(1)
        for u in range(G):
            mm_lv(u, wide=True)
        ev_h(2)
        ev_h(3)
        q_h(2)
        q_h(3)
        for g in range(NG):
            if g + 2 < NG:
                tr_h(2 * g + 4)
                tr_h(2 * g + 5)
                if g + 5 < NG:
                    load_h(g + 5)
                if g == 0:
                    load_w("mu", enc_w_out[:, 0:D])
                if g == 2:
                    load_w("dec", dec_w_in)
                if g + 5 == NG:
                    nc.sync.dma_start(out=b_mu[:], in_=enc_b_out[0:D].partition_broadcast(P))
                    nc.sync.dma_start(out=b_dec[:], in_=dec_b_in.partition_broadcast(P))
                    nc.sync.dma_start(out=g_row[0:1, :], in_=dec_ln_g.rearrange("(o n) -> o n", o=1))
                    nc.sync.dma_start(out=b_row[0:1, :], in_=dec_ln_b.rearrange("(o n) -> o n", o=1))
            if g + 2 < NG:
                ev_h(2 * g + 4)
                ev_h(2 * g + 5)
                q_h(2 * g + 4)
                q_h(2 * g + 5)
            if 1 <= g < 3:
                regroup_w("mu", g - 1)
            elif 3 <= g < 5:
                regroup_w("dec", g - 3)
            if g == 3:
                quant_w(wgs["mu"], w1c[:, 0:D], w1s[:, 0:D])
            if g == 5:
                quant_w(wgs["dec"], w2c[:], w2s[:])
            for n in range(G):
                if g >= NG - 2:
                    for q in range(1 + n % 2):
                        mm_mu(mus[0])
                        next_mu()
                exp_lv(G * g + n)
                if g + 1 < NG:
                    mm_lv(G * (g + 1) + n, wide=True)
            if g == 5:
                load_n(0)
            if g == 6:
                load_n(1)

        srow = {}
        sn = {}
        zt = {}
        zb = {}
        zps = {}
        zg = {}
        pps = {}

        def ln1(u):
            nc.scalar.activation(out=pair(u), in_=pair(u), func=ACT.Ln, bias=floor_t[:], scale=math.exp(-SCALE_EPS))

        def guard(u):
            n = u % G
            dst = et[u // G][:, n, :]
            nc.vector.scalar_tensor_tensor(
                out=dst, in0=lvp[u][:], scalar=bcol2[:, n : n + 1], in1=dst, op0=ALU.add, op1=ALU.min
            )

        def tr_s(i):
            srow[i] = ps_sr.tile([P, D], F32, name="srow", tag="sr")
            for n in range(G):
                nc.tensor.transpose(
                    srow[i][:, n * P : (n + 1) * P], et[i // G][:, n, (i % G) * P : (i % G + 1) * P], ident[:]
                )

        def kl_scale_sums(i):
            nc.scalar.activation(out=junk[0][:], in_=srow[i][:], func=ACT.Ln, scale=-1.0, accum_out=sumln[:, i : i + 1])
            nc.scalar.activation(out=junk[1][:], in_=srow[i][:], func=ACT.Square, accum_out=sums2[:, i : i + 1])

        def kl_mu_sum_v(i):
            nc.vector.scalar_tensor_tensor(
                out=junk_v[:], in0=mu[i][:], scalar=1.0, in1=mu[i][:], op0=ALU.mult, op1=ALU.mult, accum_out=summu[:, i : i + 1]
            )

        def kl_mu_sum(i):
            nc.scalar.activation(out=junk[2][:], in_=mu[i][:], func=ACT.Square, accum_out=summu[:, i : i + 1])

        def scale_noise(i):
            sn[i] = snp.tile([P, D], F32, name="sn")
            nc.vector.tensor_tensor(out=sn[i][:], in0=nch[i // G][:, i % G, :], in1=srow[i][:], op=ALU.mult)

        def sample(i):
            if i % 2 == 0:
                zt[i // 2] = grp.tile([P, 2, D], F32, name="zt")
            nc.gpsimd.tensor_tensor(out=zt[i // 2][:, i % 2, :], in0=mu[i][:], in1=sn[i][:], op=ALU.subtract)

        def round_z(j):
            nc.sync.dma_start(out=z_v[:, 2 * j : 2 * j + 2, :], in_=zt[j][:])
            zb[j] = grp.tile([P, 2, D], BF16, name="zb", align_bytes=64)
            nc.gpsimd.tensor_scalar(out=zb[j][:], in0=zt[j][:], scalar1=1.0, scalar2=0.0, op0=ALU.mult, op1=ALU.add)

        def tr_z(j):
            zps[j] = ps_1.tile([P, 4, P], F32, name="zps", tag="z")
            for jj in range(2):
                tr_words(zps[j][:, 2 * jj : 2 * jj + 2, :], zb[j][:, jj, :])

        def ev_z(j):
            zg[j] = grp.tile([P, 2, P, 2], F32, name="zg", align_bytes=64)
            src = zps[j][:].rearrange("p (j u) r -> p j r u", u=2)
            if j % 2 == 1:
                nc.scalar.copy(out=zg[j][:], in_=src)
            else:
                nc.vector.tensor_copy(out=zg[j][:], in_=src)

        def q_z(j):
            cols = slice(2 * j * P, (2 * j + 2) * P)
            nc.vector.quantize_mx(
                out=hc[:, cols].bitcast(FP8X4), scales=hs[:, cols], in_=zg[j][:].rearrange("p j r u -> p (j r u)").bitcast(BF16)
            )

        def mm2(i):
            late = i >= 17 and i % 2 == 1
            pps[i] = ps_1.tile([P, D], F32, name="acc2", tag="mu" if late else "mm2")
            cols = slice(i * P, (i + 1) * P)
            mx(pps[i][:], hc[:, cols], hs[:, cols], w2c[:], w2s[:])

        NEG = 4
        have_mean = set()

        def pre_add(i):
            nc.vector.scalar_tensor_tensor(
                out=xrow(i), in0=b_dec[:], scalar=0.0, in1=pps[i][:], op0=ALU.add, op1=ALU.add, accum_out=sumpre[:, i : i + 1]
            )

        def mean(i):
            if i % NEG == NEG - 1:
                cols = slice(i + 1 - NEG, i + 1)
                nc.gpsimd.tensor_scalar(
                    out=negmean[:, cols], in0=sumpre[:, cols], scalar1=-1.0 / D, scalar2=0.0, op0=ALU.mult, op1=ALU.add
                )
                for t in range(i + 1 - NEG, i + 1):
                    have_mean.add(t)

        gb_ps = {}

        def spread_gb():
            for name, row in (("g", g_row), ("b", b_row)):
                gb_ps[name] = ps_lv.tile([P, D], F32, name="gb_ps", tag="lv")
                nc.tensor.matmul(out=gb_ps[name][:], lhsT=ones[:], rhs=row[:], start=True, stop=True)

        def deviations(i):
            assert i in have_mean
            nc.scalar.activation(
                out=junk[i % 4][:], in_=xrow(i), func=ACT.Square, bias=negmean[:, i : i + 1], accum_out=sumdev[:, i : i + 1]
            )

        def group_rstd(i):
            if i % G == G - 1:
                cols = slice(i + 1 - G, i + 1)
                nc.gpsimd.tensor_scalar(
                    out=varep[:, cols], in0=sumdev[:, cols], scalar1=1.0 / D, scalar2=LN_EPS, op0=ALU.mult, op1=ALU.add
                )
                nc.gpsimd.tensor_tensor(out=rstd[:, cols], in0=varep[:, cols], in1=mhalf[:], op=ALU.pow)

        def centre(i):
            nc.vector.scalar_tensor_tensor(
                out=xrow(i), in0=xrow(i), scalar=negmean[:, i : i + 1], in1=gb_ps["g"][:], op0=ALU.add, op1=ALU.mult
            )

        diag = {}
        yps = {}

        def make_diag(i):
            diag[i] = dgp.tile([P, P], F32, name="diag")
            nc.gpsimd.tensor_scalar(
                out=diag[i][:], in0=ident[:], scalar1=rstd[:, i : i + 1], scalar2=0.0, op0=ALU.mult, op1=ALU.add
            )

        def affine_t(i):
            yps[i] = ps_sr.tile([P, D], F32, name="yps", tag="sr")
            nc.tensor.matmul(out=yps[i][:], lhsT=ones[:], rhs=b_row[:], start=True, stop=False)
            nc.tensor.matmul(out=yps[i][:], lhsT=diag[i][:], rhs=xrow(i), start=False, stop=True)

        def affine(i):
            nc.vector.scalar_tensor_tensor(
                out=xrow(i), in0=xrow(i), scalar=rstd[:, i : i + 1], in1=gb_ps["b"][:], op0=ALU.mult, op1=ALU.add
            )

        def silu_store(i):
            if i == NT - 2:
                for t in (i, i + 1):
                    nc.scalar.activation(out=xrow(t), in_=xrow(t), func=ACT.Silu)
                    nc.sync.dma_start(out=d_v[:, t, :], in_=xrow(t))
                return
            if on_t(i) or on_t(i + 1):
                for t in (i, i + 1):
                    nc.scalar.activation(out=xrow(t), in_=yps[t][:] if on_t(t) else xrow(t), func=ACT.Silu)
            else:
                nc.scalar.activation(out=pair(i), in_=pair(i), func=ACT.Silu)
            nc.sync.dma_start(out=d_v[:, i : i + 2, :], in_=et[i // G][:, i % G : i % G + 2, :])

        LEAD_C = 2
        LEAD_A = 7
        LEAD_S = 12

        def on(i):
            return 0 <= i < NT

        LEAD_D = 6
        LEAD_T = 10

        def on_t(i):
            return 4 <= i < NT - 2 and i % 2 == 0

        def step3(n):
            if on(n):
                deviations(n)
            if on(n - LEAD_C):
                centre(n - LEAD_C)
            if on(n - 2):
                group_rstd(n - 2)
            if on_t(n - LEAD_D):
                make_diag(n - LEAD_D)
            if on_t(n - LEAD_T):
                affine_t(n - LEAD_T)
            if on(n - LEAD_A) and not on_t(n - LEAD_A):
                affine(n - LEAD_A)
            m = n - LEAD_S
            if on(m) and m % 2 == 0:
                silu_store(m)

        steps = [0]

        def run_steps(count):
            for q in range(count):
                step3(steps[0])
                steps[0] += 1

        FILL = 8
        MU_V = 6
        DRAIN = 8
        for k in range(-FILL, NT + DRAIN):
            if k == 4:
                mu_tags.remove("z")
            if k == 6:
                mu_tags.remove("mm2")
            if k >= 0 and on(mus[0]):
                mm_mu(mus[0])
            if 0 <= k < 5:
                mm_mu(mus[0] + 1)
            if on(k + 6):
                mm_lv(k + 6)
            if on(k - 7):
                mm2(k - 7)
            if k % 2 == 0 and on(k - 4):
                tr_z((k - 4) // 2)
            if on(k + 1):
                tr_s(k + 1)
            if on(k):
                kl_scale_sums(k)
            if k == -FILL:
                for q in range(0, 8, 2):
                    ln1(q)
            elif k % 2 == 0 and on(k + 14):
                ln1(k + 14)
            if on(k - 8):
                mean(k - 8)
            if on(k + 5):
                guard(k + 5)
            if 0 <= k + 5 < MU_V:
                kl_mu_sum_v(k + 5)
            if on(k - 1):
                scale_noise(k - 1)
            if k % 2 == 1 and on(k - 5):
                ev_z((k - 5) // 2)
            if k % 2 == 0 and on(k - 6):
                q_z((k - 6) // 2)
            if on(k - 1):
                sample(k - 1)
                if k % 2 == 0:
                    round_z((k - 2) // 2)
            if k % G == 1 and 2 <= k // G + 2 < NG:
                load_n(k // G + 2)
            if k >= 0:
                next_mu()
            if 0 <= k < 5:
                next_mu()
            if on(k - 7):
                pre_add(k - 7)
            if MU_V <= k + 5 < NT:
                kl_mu_sum(k + 5)
            if k == NT - 5:
                spread_gb()
            if k >= NT:
                run_steps(3)
            elif k >= NT - 6:
                run_steps(1)

        nc.gpsimd.tensor_tensor(out=kl_a[:], in0=sums2[:], in1=summu[:], op=ALU.add)
        nc.gpsimd.tensor_scalar(out=kl_b[:], in0=kl_a[:], scalar1=0.5, scalar2=-0.5 * D, op0=ALU.mult, op1=ALU.add)
        nc.gpsimd.tensor_tensor(out=kl_c[:], in0=kl_b[:], in1=sumln[:], op=ALU.subtract)
        nc.sync.dma_start(out=kl_v, in_=kl_c[:])

        run_steps(NT + LEAD_S - steps[0])
